import numpy as np
import ml_dtypes


def mxq(x, axis, fmt="e4m3"):
    dtype, down = {"e4m3": (ml_dtypes.float8_e4m3fn, 7), "e5m2": (ml_dtypes.float8_e5m2, 14)}[fmt]
    v = np.moveaxis(np.asarray(x, np.float32).astype(ml_dtypes.bfloat16).astype(np.float64), axis, -1)
    blocks = v.reshape(v.shape[:-1] + (-1, 32))
    amax = np.abs(blocks).max(-1, keepdims=True)
    byte = np.maximum(np.where(amax > 0, np.frexp(amax)[1] - 1 + 127, 0) - down, 1)
    scale = np.exp2(byte - 127.0)
    codes = (blocks / scale).astype(np.float32).astype(dtype).astype(np.float64)
    return np.moveaxis((codes * scale).reshape(v.shape), -1, axis)


WIDE = False


def mx_kscale(k):
    if not WIDE:
        return np.ones(k)
    levels = np.array([10, -10, 5, -5, 0])
    a = np.random.permutation(np.resize(levels, k // 512 * 4)).reshape(k // 512, 4)
    idx = np.arange(k)
    return np.exp2(a[idx // 512, idx % 128 // 32])


BF16 = ml_dtypes.bfloat16


def bf(x):
    return np.asarray(x, np.float32).astype(BF16)


def f64(x):
    return np.asarray(x).astype(np.float64)


N, T, U, H, J, V = 4, 64, 32, 512, 1024, 512
TEMP = 1.0


def log_softmax(v):
    d = v - v.max(-1, keepdims=True)
    return d - np.log(np.exp(d).sum(-1, keepdims=True))


def setup_inputs():
    s = mx_kscale(2 * H)
    return {"h_pred": bf(np.random.standard_normal((N, U, H)) * s[:H]),
            "h_enc": bf(np.random.standard_normal((N, T, H)) * s[H:]),
            "W1": bf(np.random.standard_normal((2 * H, J)) / np.sqrt(2 * H) / s[:, None]),
            "b1": bf(np.random.standard_normal(J) * 0.1),
            "W2": bf(np.random.standard_normal((J, V)) * 2.0 / np.sqrt(J)),
            "b2": bf(np.random.standard_normal(V) * 0.1)}


def reference(h_pred, h_enc, W1, b1, W2, b2):
    H_p = h_pred.shape[-1]
    w1q = mxq(f64(W1), 0, "e4m3")
    pred_proj = mxq(f64(h_pred), 2, "e4m3") @ w1q[:H_p]
    enc_proj = mxq(f64(h_enc), 2, "e4m3") @ w1q[H_p:]
    z = pred_proj[:, None, :, :] + enc_proj[:, :, None, :] + f64(b1)
    x = np.tanh(z)
    logits = (mxq(x, 3, "e4m3") @ mxq(f64(W2), 0, "e4m3")) + f64(b2)
    return log_softmax(logits / TEMP)

@@ -1,0 +1,403 @@
+from contextlib import ExitStack
+
+import concourse.mybir as mybir
+from concourse.masks import make_identity
+
+FLOPS = 2 * (128 * 512 * 1024 + 256 * 512 * 1024 + 8192 * 1024 * 512)
+
+BF16 = mybir.dt.bfloat16
+F32 = mybir.dt.float32
+U32 = mybir.dt.uint32
+I32 = mybir.dt.int32
+U8 = mybir.dt.uint8
+FP8X4 = mybir.dt.float8_e4m3fn_x4
+ACT = mybir.ActivationFunctionType
+ALU = mybir.AluOpType
+AX = mybir.AxisListType
+
+P = 128
+BLOCKS = 16
+LN_AFTER = (4, 9, 12, 14, 15)
+ON_VECTOR = (14, 15)
+W1_PIECES = ((0, 256), (256, 256), (512, 512))
+HE_PIECES = ((0, 32), (32, 32), (64, 64), (128, 128))
+FINE = (14, 15)
+
+
+def regroup(engine_copy, dst, src):
+    engine_copy(
+        out=dst.rearrange("p (c i) t -> p c t i", i=4),
+        in_=src.rearrange("p t (c i) -> p c t i", i=4),
+    )
+
+
+def tile_joint_t_kernel(tc, h_pred, h_enc, W1, b1, W2, b2, out):
+    nc = tc.nc
+    out_rows = out.flatten_outer_dims()
+    with ExitStack() as ctx:
+        ctx.enter_context(tc.manual_schedule())
+        const = ctx.enter_context(tc.tile_pool(name="const", bufs=1))
+        prep = ctx.enter_context(tc.tile_pool(name="prep", bufs=1))
+        loop = ctx.enter_context(tc.tile_pool(name="loop", bufs=2))
+        lpool = ctx.enter_context(tc.tile_pool(name="lpool", bufs=9))
+
+        b1t = prep.tile([P, P], BF16)
+        nc.vector.memset(b1t[:], 0.0)
+        warm = const.tile([P, 1], F32)
+        nc.vector.memset(warm[:], 0.0)
+        hp_s = const.tile([P, 128], U8, align_bytes=64)
+        he4_s = const.tile([P, 1024], U8, align_bytes=64)
+        nc.vector.memset(hp_s[:].bitcast(I32), 0)
+        nc.vector.memset(he4_s[:].bitcast(I32), 0)
+
+        he_sb = prep.tile([P, 2, 512], BF16)
+        nc.sync.dma_start(out=he_sb[:], in_=h_enc.flatten_outer_dims().rearrange("(a p) k -> p a k", p=P))
+        hp_sb = prep.tile([P, 512], BF16)
+        nc.sync.dma_start(out=hp_sb[:], in_=h_pred.flatten_outer_dims())
+        nc.sync.dma_start(out=b1t[0:8, :], in_=b1.rearrange("(c p) -> c p", p=P))
+        w1raw = {}
+        for h, (j0, jw) in enumerate(W1_PIECES):
+            for g in range(2):
+                raw = prep.tile([P, 4, jw], BF16, name="w1raw%d%d" % (g, h))
+                nc.sync.dma_start(
+                    out=raw[:],
+                    in_=W1[512 * g : 512 * (g + 1), j0 : j0 + jw].rearrange("(t p) j -> p t j", p=P),
+                )
+                w1raw[(g, h)] = raw
+        w2raw = {}
+        for g in range(2):
+            raw = prep.tile([P, 4, 512], BF16, tag="w2raw", bufs=2, name="w2raw%d" % g)
+            nc.sync.dma_start(out=raw[:], in_=W2[512 * g : 512 * (g + 1), :].rearrange("(t p) v -> p t v", p=P))
+            w2raw[g] = raw
+        b2b = prep.tile([P, 512], BF16)
+        nc.sync.dma_start(out=b2b[:], in_=b2.partition_broadcast(P))
+
+        warm2 = const.tile([P, 1], F32)
+        nc.scalar.activation(out=warm2[:], in_=warm[:], func=ACT.Tanh)
+        ident = const.tile([P, P], BF16)
+        make_identity(nc, ident[:])
+
+        w1c = const.tile([P, 2, 1024], U32, align_bytes=64)
+        w1s = const.tile([P, 2, 1024], U8, align_bytes=64)
+        w2c = const.tile([P, 2, 512], U32, align_bytes=64)
+        w2s = const.tile([P, 2, 512], U8, align_bytes=64)
+        hp_c = const.tile([P, 128], U32, align_bytes=64)
+        he4_c = const.tile([P, 1024], U32, align_bytes=64)
+        b1_sb = const.tile([P, 8], F32)
+        b2f = const.tile([P, 512], F32)
+        negm = const.tile([P, 64], F32)
+        ssum = const.tile([P, 64], F32)
+        lns = const.tile([P, 64], F32)
+        negc = const.tile([P, 64], F32)
+
+        he_g = prep.tile([P, 256, 4, 4], BF16, align_bytes=64)
+        he_lin = prep.tile([P, 2, 4, P], BF16)
+        hp_g = prep.tile([P, P, 4], BF16, align_bytes=64)
+        w1g = {}
+        for h, (j0, jw) in enumerate(W1_PIECES):
+            for g in range(2):
+                w1g[(g, h)] = prep.tile([P, jw, 4], BF16, align_bytes=64, name="w1g%d%d" % (g, h))
+        with tc.psum_pool(name="pps", bufs=1) as pps:
+            heT = pps.tile([P, 2, 4, P], BF16)
+            hpT = pps.tile([P, 4, P], BF16)
+            b1T = pps.tile([P, P], BF16)
+            for t in range(4):
+                nc.tensor.transpose(heT[:, 0, t, :], he_sb[:, 0, P * t : P * (t + 1)], ident[:])
+            for t in range(4):
+                nc.tensor.transpose(hpT[:, t, :], hp_sb[:, P * t : P * (t + 1)], ident[:])
+            nc.tensor.transpose(b1T[:], b1t[:], ident[:])
+            for t in range(4):
+                nc.tensor.transpose(heT[:, 1, t, :], he_sb[:, 1, P * t : P * (t + 1)], ident[:])
+            nc.scalar.copy(out=he_lin[:, 0], in_=heT[:, 0])
+            nc.scalar.copy(out=hp_g[:], in_=hpT[:].rearrange("p t r -> p r t"))
+            nc.scalar.copy(out=b1_sb[:], in_=b1T[:, 0:8])
+            regroup(nc.scalar.copy, w1g[(1, 0)][:], w1raw[(1, 0)][:])
+            nc.scalar.copy(out=he_lin[:, 1], in_=heT[:, 1])
+            regroup(nc.scalar.copy, w1g[(1, 1)][:], w1raw[(1, 1)][:])
+
+        def he_views(piece):
+            r0, nr = HE_PIECES[piece]
+            a, q0 = r0 // P, r0 % P
+            dst = he_g[:, r0 : r0 + nr, :, :]
+            src = (
+                he_lin[:, a, :, q0 : q0 + nr].rearrange("p t r -> p r t").unsqueeze(2).to_broadcast([P, nr, 4, 4])
+            )
+            return dst, src
+
+        def gp_copy(dst, src):
+            nc.gpsimd.tensor_scalar(out=dst, in0=src, scalar1=1.0, scalar2=0.0, op0=ALU.mult, op1=ALU.add)
+
+        def quant_he(piece):
+            r0, nr = HE_PIECES[piece]
+            nc.vector.quantize_mx(
+                out=he4_c[:, 4 * r0 : 4 * (r0 + nr)].bitcast(FP8X4),
+                scales=he4_s[:, 4 * r0 : 4 * (r0 + nr)],
+                in_=he_g[:, r0 : r0 + nr].rearrange("p r e t -> p (r e t)"),
+            )
+
+        pf = {}
+        eb = {}
+
+        def moves(b):
+            if b >= BLOCKS:
+                return
+            n = b // 4
+            if b % 4 == 0:
+                pf_c = const.tile([P, 512], U32, align_bytes=64, name="pfc%d" % n)
+                pf_s = const.tile([P, 512], U8, align_bytes=64, name="pfs%d" % n)
+                nc.vector.tensor_copy(
+                    out=pf_c[:].bitcast(I32).rearrange("p (a u) -> p a u", u=32),
+                    in_=hp_c[:, 32 * n : 32 * (n + 1)].bitcast(I32).unsqueeze(1).to_broadcast([P, 16, 32]),
+                )
+                nc.vector.tensor_copy(
+                    out=pf_s[:].bitcast(I32).rearrange("p (a u) -> p a u", u=8),
+                    in_=hp_s[:, 32 * n : 32 * (n + 1)].bitcast(I32).unsqueeze(1).to_broadcast([P, 16, 8]),
+                )
+                pf[n] = (pf_c, pf_s)
+            eb_c = loop.tile([P, 512], U32, align_bytes=64, tag="ebc", bufs=3, name="ebc%d" % b)
+            eb_s = loop.tile([P, 512], U8, align_bytes=64, tag="ebs", bufs=3, name="ebs%d" % b)
+            nc.vector.tensor_copy(
+                out=eb_c[:].bitcast(I32).rearrange("p (t a w) -> p t a w", a=8, w=4),
+                in_=he4_c[:, 64 * b : 64 * (b + 1)]
+                .bitcast(I32)
+                .rearrange("p (t w) -> p t w", w=4)
+                .unsqueeze(2)
+                .to_broadcast([P, 16, 8, 4]),
+            )
+            nc.vector.tensor_copy(
+                out=eb_s[:].bitcast(I32).rearrange("p (t a) -> p t a", a=8),
+                in_=he4_s[:, 64 * b : 64 * (b + 1)].bitcast(I32).unsqueeze(2).to_broadcast([P, 16, 8]),
+            )
+            eb[b] = (eb_c, eb_s)
+
+        def quant_w1(g, h):
+            j0, jw = W1_PIECES[h]
+            nc.vector.quantize_mx(
+                out=w1c[:, g, j0 : j0 + jw].bitcast(FP8X4),
+                scales=w1s[:, g, j0 : j0 + jw],
+                in_=w1g[(g, h)][:].rearrange("p w t -> p (w t)"),
+            )
+
+        dst, src = he_views(0)
+        nc.vector.tensor_copy(out=dst, in_=src)
+        regroup(nc.vector.tensor_copy, w1g[(0, 0)][:], w1raw[(0, 0)][:])
+        quant_he(0)
+        nc.vector.quantize_mx(
+            out=hp_c[:].bitcast(FP8X4), scales=hp_s[:], in_=hp_g[:].rearrange("p r t -> p (r t)")
+        )
+        quant_w1(0, 0)
+        moves(0)
+        quant_w1(1, 0)
+        regroup(nc.vector.tensor_copy, w1g[(0, 1)][:], w1raw[(0, 1)][:])
+        for piece in (1, 2):
+            dst, src = he_views(piece)
+            gp_copy(dst, src)
+        gp_copy(w1g[(1, 2)][:], w1raw[(1, 2)][:].rearrange("p t w -> p w t"))
+        w2g = {}
+        for g in range(2):
+            w2g[g] = prep.tile([P, 512, 4], BF16, tag="w2g", bufs=2, align_bytes=64, name="w2g%d" % g)
+        gp_copy(w2g[1][:], w2raw[1][:].rearrange("p t w -> p w t"))
+        gp_copy(b2f[:], b2b[:])
+        dst, src = he_views(3)
+        gp_copy(dst, src)
+        quant_w1(0, 1)
+        quant_w1(1, 1)
+        regroup(nc.vector.tensor_copy, w1g[(0, 2)][:], w1raw[(0, 2)][:])
+        moves(1)
+        quant_w1(0, 2)
+        quant_w1(1, 2)
+
+        zps = ctx.enter_context(tc.psum_pool(name="zps", bufs=4))
+        lps = ctx.enter_context(tc.psum_pool(name="lps", bufs=4))
+
+        xps = {}
+        xgs = {}
+        xq = {}
+        accs = {}
+        ltiles = {}
+
+        def z_tanh(s):
+            pf_c, pf_s = pf[s // 4]
+            eb_c, eb_s = eb[s]
+            for g in range(2):
+                xp = loop.tile([P, 4, 512], BF16, tag="xp", bufs=4, name="xp%d_%d" % (s, g))
+                xps[(s, g)] = xp
+                for tq in range(4):
+                    c = 4 * g + tq
+                    cols = slice(P * c, P * (c + 1))
+                    zt = zps.tile([P, 512], F32, tag="z", name="z%d_%d" % (s, c))
+                    nc.tensor.matmul_mx(
+                        out=zt[:],
+                        lhsT=w1c[:, 0, cols].bitcast(FP8X4),
+                        lhsT_scale=w1s[:, 0, cols],
+                        rhs=pf_c[:].bitcast(FP8X4),
+                        rhs_scale=pf_s[:],
+                        start=True,
+                        stop=False,
+                    )
+                    nc.tensor.matmul_mx(
+                        out=zt[:],
+                        lhsT=w1c[:, 1, cols].bitcast(FP8X4),
+                        lhsT_scale=w1s[:, 1, cols],
+                        rhs=eb_c[:].bitcast(FP8X4),
+                        rhs_scale=eb_s[:],
+                        start=False,
+                        stop=True,
+                    )
+                    nc.scalar.activation(
+                        out=xp[:, tq, :], in_=zt[:], func=ACT.Tanh, bias=b1_sb[:, c : c + 1], scale=1.0
+                    )
+
+        def logits(b):
+            xc, xs = xq[b]
+            for r in range(4):
+                rows = slice(P * r, P * (r + 1))
+                acc = lps.tile([P, 512], F32, tag="lg", name="lg%d_%d" % (b, r))
+                accs[(b, r)] = acc
+                for g in range(2):
+                    nc.tensor.matmul_mx(
+                        out=acc[:],
+                        lhsT=xc[:, g, rows].bitcast(FP8X4),
+                        lhsT_scale=xs[:, g, rows],
+                        rhs=w2c[:, g, :].bitcast(FP8X4),
+                        rhs_scale=w2s[:, g, :],
+                        start=(g == 0),
+                        stop=(g == 1),
+                    )
+
+        def exps(b):
+            lt = ltiles[b]
+            for r in range(4):
+                i = 4 * b + r
+                junk = loop.tile([P, 512], BF16, tag="junk", bufs=2, name="junk%d" % i)
+                nc.scalar.activation(
+                    out=junk[:],
+                    in_=lt[:, r, :],
+                    func=ACT.Exp,
+                    bias=negm[:, i : i + 1],
+                    scale=1.0,
+                    accum_out=ssum[:, i : i + 1],
+                )
+
+        def v_regroup(s, g):
+            if s >= BLOCKS:
+                return
+            xg = loop.tile([P, 512, 4], BF16, tag="xg", bufs=2, align_bytes=64, name="xg%d_%d" % (s, g))
+            xgs[(s, g)] = xg
+            regroup(nc.vector.tensor_copy, xg[:], xps[(s, g)][:])
+
+        def v_quant(s, g):
+            if s >= BLOCKS:
+                return
+            if g == 0:
+                xc = loop.tile([P, 2, 512], U32, align_bytes=64, tag="xc", bufs=2, name="xc%d" % s)
+                xs = loop.tile([P, 2, 512], U8, align_bytes=64, tag="xs", bufs=2, name="xs%d" % s)
+                xq[s] = (xc, xs)
+            xc, xs = xq[s]
+            nc.vector.quantize_mx(
+                out=xc[:, g, :].bitcast(FP8X4),
+                scales=xs[:, g, :],
+                in_=xgs[(s, g)][:].rearrange("p w t -> p (w t)"),
+            )
+
+        def v_bias(b, r):
+            if b < 0:
+                return
+            if r == 0:
+                ltiles[b] = lpool.tile([P, 4, 512], F32, tag="L", name="L%d" % b)
+            nc.vector.tensor_tensor(out=ltiles[b][:, r, :], in0=accs[(b, r)][:], in1=b2f[:], op=ALU.add)
+
+        def v_max_tile(b, r):
+            if b in FINE:
+                i = 4 * b + r
+                nc.vector.tensor_reduce(
+                    out=negm[:, i : i + 1], in_=ltiles[b][:, r, :], axis=AX.X, op=ALU.max, negate=True
+                )
+
+        def v_max_block(b):
+            if b >= 0 and b not in FINE:
+                nc.vector.tensor_reduce(
+                    out=negm[:, 4 * b : 4 * (b + 1)], in_=ltiles[b][:], axis=AX.X, op=ALU.max, negate=True
+                )
+
+        batch_start = 0
+        for s in range(BLOCKS + 2):
+            if s < BLOCKS:
+                z_tanh(s)
+            if s == 0:
+                regroup(nc.scalar.copy, w2g[0][:], w2raw[0][:])
+            if 1 <= s <= BLOCKS:
+                logits(s - 1)
+            if s >= 2:
+                exps(s - 2)
+            if s <= BLOCKS:
+                b = s - 1
+                v_regroup(s, 0)
+                v_bias(b, 0)
+                v_quant(s, 0)
+                v_bias(b, 1)
+                v_max_tile(b, 0)
+                v_regroup(s, 1)
+                v_bias(b, 2)
+                v_max_tile(b, 1)
+                v_quant(s, 1)
+                v_bias(b, 3)
+                v_max_tile(b, 2)
+                v_max_tile(b, 3)
+                v_max_block(b)
+                if s == 0:
+                    quant_he(1)
+                    quant_he(2)
+                    for g in (1, 0):
+                        nc.vector.quantize_mx(
+                            out=w2c[:, g, :].bitcast(FP8X4),
+                            scales=w2s[:, g, :],
+                            in_=w2g[g][:].rearrange("p w t -> p (w t)"),
+                        )
+                if s == 1:
+                    quant_he(3)
+                moves(s + 2)
+            if s - 2 in LN_AFTER:
+                last = s - 2
+                lo, hi = 4 * batch_start, 4 * (last + 1)
+                nc.scalar.activation(out=lns[:, lo:hi], in_=ssum[:, lo:hi], func=ACT.Ln)
+                gp_blocks = [bb for bb in range(batch_start, last + 1) if bb not in ON_VECTOR]
+                if gp_blocks:
+                    glo, ghi = 4 * gp_blocks[0], 4 * (gp_blocks[-1] + 1)
+                    nc.gpsimd.tensor_tensor(
+                        out=negc[:, glo:ghi], in0=negm[:, glo:ghi], in1=lns[:, glo:ghi], op=ALU.subtract
+                    )
+                for bb in range(batch_start, last + 1):
+                    lt = ltiles[bb]
+                    if bb not in ON_VECTOR:
+                        for r in range(4):
+                            i = 4 * bb + r
+                            nc.gpsimd.tensor_scalar(
+                                out=lt[:, r, :],
+                                in0=lt[:, r, :],
+                                scalar1=1.0,
+                                scalar2=negc[:, i : i + 1],
+                                op0=ALU.mult,
+                                op1=ALU.add,
+                            )
+                        nc.sync.dma_start(
+                            out=out_rows[512 * bb : 512 * (bb + 1), :].rearrange("(r p) v -> p r v", p=P), in_=lt[:]
+                        )
+                    else:
+                        for q in range(2):
+                            for r in (2 * q, 2 * q + 1):
+                                i = 4 * bb + r
+                                nc.vector.tensor_scalar(
+                                    out=lt[:, r, :],
+                                    in0=lt[:, r, :],
+                                    scalar1=negm[:, i : i + 1],
+                                    scalar2=lns[:, i : i + 1],
+                                    op0=ALU.add,
+                                    op1=ALU.subtract,
+                                )
+                            base = 512 * bb + 256 * q
+                            nc.sync.dma_start(
+                                out=out_rows[base : base + 256, :].rearrange("(r p) v -> p r v", p=P),
+                                in_=lt[:, 2 * q : 2 * q + 2, :],
+                            )
+                batch_start = last + 1

@@ -17,9 +17,9 @@ AX = mybir.AxisListType
 
 P = 128
 BLOCKS = 16
-LN_AFTER = (4, 9, 12, 14, 15)
+LN_AFTER = (5, 11, 13, 14, 15)
 ON_VECTOR = (14, 15)
-W1_PIECES = ((0, 256), (256, 256), (512, 512))
+W1_PIECES = ((0, 256), (256, 256), (512, 256), (768, 256))
 HE_PIECES = ((0, 32), (32, 32), (64, 64), (128, 128))
 FINE = (14, 15)
 
@@ -46,9 +46,8 @@ def tile_joint_t_kernel(tc, h_pred, h_enc, W1, b1, W2, b2, out):
         warm = const.tile([P, 1], F32)
         nc.vector.memset(warm[:], 0.0)
         hp_s = const.tile([P, 128], U8, align_bytes=64)
-        he4_s = const.tile([P, 1024], U8, align_bytes=64)
+        he8_s = const.tile([P, 2048], U8, align_bytes=64)
         nc.vector.memset(hp_s[:].bitcast(I32), 0)
-        nc.vector.memset(he4_s[:].bitcast(I32), 0)
 
         he_sb = prep.tile([P, 2, 512], BF16)
         nc.sync.dma_start(out=he_sb[:], in_=h_enc.flatten_outer_dims().rearrange("(a p) k -> p a k", p=P))
@@ -82,7 +81,7 @@ def tile_joint_t_kernel(tc, h_pred, h_enc, W1, b1, W2, b2, out):
         w2c = const.tile([P, 2, 512], U32, align_bytes=64)
         w2s = const.tile([P, 2, 512], U8, align_bytes=64)
         hp_c = const.tile([P, 128], U32, align_bytes=64)
-        he4_c = const.tile([P, 1024], U32, align_bytes=64)
+        he8_c = const.tile([P, 2048], U32, align_bytes=64)
         b1_sb = const.tile([P, 8], F32)
         b2f = const.tile([P, 512], F32)
         negm = const.tile([P, 64], F32)
@@ -90,7 +89,7 @@ def tile_joint_t_kernel(tc, h_pred, h_enc, W1, b1, W2, b2, out):
         lns = const.tile([P, 64], F32)
         negc = const.tile([P, 64], F32)
 
-        he_g = prep.tile([P, 256, 4, 4], BF16, align_bytes=64)
+        he_g = prep.tile([P, 256, 8, 4], BF16, align_bytes=64)
         he_lin = prep.tile([P, 2, 4, P], BF16)
         hp_g = prep.tile([P, P, 4], BF16, align_bytes=64)
         w1g = {}
@@ -120,7 +119,7 @@ def tile_joint_t_kernel(tc, h_pred, h_enc, W1, b1, W2, b2, out):
             a, q0 = r0 // P, r0 % P
             dst = he_g[:, r0 : r0 + nr, :, :]
             src = (
-                he_lin[:, a, :, q0 : q0 + nr].rearrange("p t r -> p r t").unsqueeze(2).to_broadcast([P, nr, 4, 4])
+                he_lin[:, a, :, q0 : q0 + nr].rearrange("p t r -> p r t").unsqueeze(2).to_broadcast([P, nr, 8, 4])
             )
             return dst, src
 
@@ -130,45 +129,36 @@ def tile_joint_t_kernel(tc, h_pred, h_enc, W1, b1, W2, b2, out):
         def quant_he(piece):
             r0, nr = HE_PIECES[piece]
             nc.vector.quantize_mx(
-                out=he4_c[:, 4 * r0 : 4 * (r0 + nr)].bitcast(FP8X4),
-                scales=he4_s[:, 4 * r0 : 4 * (r0 + nr)],
+                out=he8_c[:, 8 * r0 : 8 * (r0 + nr)].bitcast(FP8X4),
+                scales=he8_s[:, 8 * r0 : 8 * (r0 + nr)],
                 in_=he_g[:, r0 : r0 + nr].rearrange("p r e t -> p (r e t)"),
             )
 
         pf = {}
-        eb = {}
 
         def moves(b):
-            if b >= BLOCKS:
+            if b >= BLOCKS or b % 4 != 0:
                 return
             n = b // 4
-            if b % 4 == 0:
-                pf_c = const.tile([P, 512], U32, align_bytes=64, name="pfc%d" % n)
-                pf_s = const.tile([P, 512], U8, align_bytes=64, name="pfs%d" % n)
-                nc.vector.tensor_copy(
-                    out=pf_c[:].bitcast(I32).rearrange("p (a u) -> p a u", u=32),
-                    in_=hp_c[:, 32 * n : 32 * (n + 1)].bitcast(I32).unsqueeze(1).to_broadcast([P, 16, 32]),
-                )
-                nc.vector.tensor_copy(
-                    out=pf_s[:].bitcast(I32).rearrange("p (a u) -> p a u", u=8),
-                    in_=hp_s[:, 32 * n : 32 * (n + 1)].bitcast(I32).unsqueeze(1).to_broadcast([P, 16, 8]),
-                )
-                pf[n] = (pf_c, pf_s)
-            eb_c = loop.tile([P, 512], U32, align_bytes=64, tag="ebc", bufs=3, name="ebc%d" % b)
-            eb_s = loop.tile([P, 512], U8, align_bytes=64, tag="ebs", bufs=3, name="ebs%d" % b)
+            pf_c = const.tile([P, 512], U32, align_bytes=64, name="pfc%d" % n)
+            pf_s = const.tile([P, 512], U8, align_bytes=64, name="pfs%d" % n)
             nc.vector.tensor_copy(
-                out=eb_c[:].bitcast(I32).rearrange("p (t a w) -> p t a w", a=8, w=4),
-                in_=he4_c[:, 64 * b : 64 * (b + 1)]
+                out=pf_c[:].bitcast(I32).rearrange("p (a t w) -> p a t w", a=4, w=8),
+                in_=hp_c[:, 32 * n : 32 * (n + 1)]
                 .bitcast(I32)
-                .rearrange("p (t w) -> p t w", w=4)
+                .rearrange("p (a w) -> p a w", w=8)
                 .unsqueeze(2)
-                .to_broadcast([P, 16, 8, 4]),
+                .to_broadcast([P, 4, 16, 8]),
             )
             nc.vector.tensor_copy(
-                out=eb_s[:].bitcast(I32).rearrange("p (t a) -> p t a", a=8),
-                in_=he4_s[:, 64 * b : 64 * (b + 1)].bitcast(I32).unsqueeze(2).to_broadcast([P, 16, 8]),
+                out=pf_s[:].bitcast(I32).rearrange("p (a t w) -> p a t w", a=4, w=2),
+                in_=hp_s[:, 32 * n : 32 * (n + 1)]
+                .bitcast(I32)
+                .rearrange("p (a w) -> p a w", w=2)
+                .unsqueeze(2)
+                .to_broadcast([P, 4, 16, 2]),
             )
-            eb[b] = (eb_c, eb_s)
+            pf[n] = (pf_c, pf_s)
 
         def quant_w1(g, h):
             j0, jw = W1_PIECES[h]
@@ -189,23 +179,26 @@ def tile_joint_t_kernel(tc, h_pred, h_enc, W1, b1, W2, b2, out):
         moves(0)
         quant_w1(1, 0)
         regroup(nc.vector.tensor_copy, w1g[(0, 1)][:], w1raw[(0, 1)][:])
-        for piece in (1, 2):
-            dst, src = he_views(piece)
-            gp_copy(dst, src)
         gp_copy(w1g[(1, 2)][:], w1raw[(1, 2)][:].rearrange("p t w -> p w t"))
+        gp_copy(w1g[(1, 3)][:], w1raw[(1, 3)][:].rearrange("p t w -> p w t"))
+        dst, src = he_views(1)
+        gp_copy(dst, src)
         w2g = {}
         for g in range(2):
             w2g[g] = prep.tile([P, 512, 4], BF16, tag="w2g", bufs=2, align_bytes=64, name="w2g%d" % g)
         gp_copy(w2g[1][:], w2raw[1][:].rearrange("p t w -> p w t"))
         gp_copy(b2f[:], b2b[:])
-        dst, src = he_views(3)
-        gp_copy(dst, src)
+        for piece in (2, 3):
+            dst, src = he_views(piece)
+            gp_copy(dst, src)
         quant_w1(0, 1)
         quant_w1(1, 1)
         regroup(nc.vector.tensor_copy, w1g[(0, 2)][:], w1raw[(0, 2)][:])
-        moves(1)
+        regroup(nc.vector.tensor_copy, w1g[(0, 3)][:], w1raw[(0, 3)][:])
         quant_w1(0, 2)
         quant_w1(1, 2)
+        quant_w1(0, 3)
+        quant_w1(1, 3)
 
         zps = ctx.enter_context(tc.psum_pool(name="zps", bufs=4))
         lps = ctx.enter_context(tc.psum_pool(name="lps", bufs=4))
@@ -218,7 +211,7 @@ def tile_joint_t_kernel(tc, h_pred, h_enc, W1, b1, W2, b2, out):
 
         def z_tanh(s):
             pf_c, pf_s = pf[s // 4]
-            eb_c, eb_s = eb[s]
+            enc = slice(P * s, P * (s + 1))
             for g in range(2):
                 xp = loop.tile([P, 4, 512], BF16, tag="xp", bufs=4, name="xp%d_%d" % (s, g))
                 xps[(s, g)] = xp
@@ -226,26 +219,32 @@ def tile_joint_t_kernel(tc, h_pred, h_enc, W1, b1, W2, b2, out):
                     c = 4 * g + tq
                     cols = slice(P * c, P * (c + 1))
                     zt = zps.tile([P, 512], F32, tag="z", name="z%d_%d" % (s, c))
-                    nc.tensor.matmul_mx(
-                        out=zt[:],
-                        lhsT=w1c[:, 0, cols].bitcast(FP8X4),
-                        lhsT_scale=w1s[:, 0, cols],
-                        rhs=pf_c[:].bitcast(FP8X4),
-                        rhs_scale=pf_s[:],
-                        start=True,
-                        stop=False,
-                    )
-                    nc.tensor.matmul_mx(
-                        out=zt[:],
-                        lhsT=w1c[:, 1, cols].bitcast(FP8X4),
-                        lhsT_scale=w1s[:, 1, cols],
-                        rhs=eb_c[:].bitcast(FP8X4),
-                        rhs_scale=eb_s[:],
-                        start=False,
-                        stop=True,
-                    )
+                    for a in range(4):
+                        part = slice(P * a, P * (a + 1))
+                        nc.tensor.matmul_mx(
+                            out=zt[:, part],
+                            lhsT=w1c[:, 0, cols].bitcast(FP8X4),
+                            lhsT_scale=w1s[:, 0, cols],
+                            rhs=pf_c[:, part].bitcast(FP8X4),
+                            rhs_scale=pf_s[:, part],
+                            start=True,
+                            stop=False,
+                        )
+                        nc.tensor.matmul_mx(
+                            out=zt[:, part],
+                            lhsT=w1c[:, 1, cols].bitcast(FP8X4),
+                            lhsT_scale=w1s[:, 1, cols],
+                            rhs=he8_c[:, enc].bitcast(FP8X4),
+                            rhs_scale=he8_s[:, enc],
+                            start=False,
+                            stop=True,
+                        )
                     nc.scalar.activation(
-                        out=xp[:, tq, :], in_=zt[:], func=ACT.Tanh, bias=b1_sb[:, c : c + 1], scale=1.0
+                        out=xp[:, tq, :].rearrange("p (t a w) -> p t a w", a=4, w=8),
+                        in_=zt[:].rearrange("p (a t w) -> p t a w", a=4, w=8),
+                        func=ACT.Tanh,
+                        bias=b1_sb[:, c : c + 1],
+                        scale=1.0,
                     )
 
         def logits(b):
@@ -333,21 +332,20 @@ def tile_joint_t_kernel(tc, h_pred, h_enc, W1, b1, W2, b2, out):
             if s <= BLOCKS:
                 b = s - 1
                 v_regroup(s, 0)
-                v_bias(b, 0)
+                v_regroup(s, 1)
                 v_quant(s, 0)
+                v_quant(s, 1)
+                v_bias(b, 0)
                 v_bias(b, 1)
                 v_max_tile(b, 0)
-                v_regroup(s, 1)
                 v_bias(b, 2)
                 v_max_tile(b, 1)
-                v_quant(s, 1)
                 v_bias(b, 3)
                 v_max_tile(b, 2)
                 v_max_tile(b, 3)
                 v_max_block(b)
                 if s == 0:
                     quant_he(1)
-                    quant_he(2)
                     for g in (1, 0):
                         nc.vector.quantize_mx(
                             out=w2c[:, g, :].bitcast(FP8X4),
@@ -355,6 +353,8 @@ def tile_joint_t_kernel(tc, h_pred, h_enc, W1, b1, W2, b2, out):
                             in_=w2g[g][:].rearrange("p w t -> p (w t)"),
                         )
                 if s == 1:
+                    quant_he(2)
+                if s == 2:
                     quant_he(3)
                 moves(s + 2)
             if s - 2 in LN_AFTER:

@@ -17,11 +17,16 @@ AX = mybir.AxisListType
 
 P = 128
 BLOCKS = 16
-LN_AFTER = (5, 11, 13, 14, 15)
-ON_VECTOR = (14, 15)
+LN_SLOPE = 355.0 / 512.0 / 2.0**23
+LN_OFFSET = -127.0 * 355.0 / 512.0 + 61.0 / 2048.0
+CUBE3 = 3.0 ** (1.0 / 3.0)
+LN_BATCHES = {6: (0, 4), 10: (4, 8), 12: (8, 10), 14: (10, 12), 16: (12, 14)}
+FINISH = {7: (0,), 8: (1,), 9: (2,), 10: (3,), 11: (4,), 12: (5, 6), 13: (7, 8), 14: (9,), 15: (10, 11)}
 W1_PIECES = ((0, 256), (256, 256), (512, 256), (768, 256))
 HE_PIECES = ((0, 32), (32, 32), (64, 64), (128, 128))
-FINE = (14, 15)
+XG_BUFS = 3
+GP_COLS = 256
+FINE = (15,)
 
 
 def regroup(engine_copy, dst, src):
@@ -86,8 +91,14 @@ def tile_joint_t_kernel(tc, h_pred, h_enc, W1, b1, W2, b2, out):
         b2f = const.tile([P, 512], F32)
         negm = const.tile([P, 64], F32)
         ssum = const.tile([P, 64], F32)
-        lns = const.tile([P, 64], F32)
-        negc = const.tile([P, 64], F32)
+        lny = const.tile([P, 64], F32)
+        lne = const.tile([P, 64], F32)
+        lnt = const.tile([P, 64], F32)
+        lnb = const.tile([P, 64], F32)
+        lng = const.tile([P, 64], F32)
+        negc_blocks = [const.tile([P, 4], F32, name="negc%d" % b) for b in range(BLOCKS)]
+        ebias = const.tile([P, 1], F32)
+        nc.vector.memset(ebias[:], -LN_OFFSET)
 
         he_g = prep.tile([P, 256, 8, 4], BF16, align_bytes=64)
         he_lin = prep.tile([P, 2, 4, P], BF16)
@@ -211,6 +222,7 @@ def tile_joint_t_kernel(tc, h_pred, h_enc, W1, b1, W2, b2, out):
 
         def z_tanh(s):
             pf_c, pf_s = pf[s // 4]
+
             enc = slice(P * s, P * (s + 1))
             for g in range(2):
                 xp = loop.tile([P, 4, 512], BF16, tag="xp", bufs=4, name="xp%d_%d" % (s, g))
@@ -246,6 +258,74 @@ def tile_joint_t_kernel(tc, h_pred, h_enc, W1, b1, W2, b2, out):
                         bias=b1_sb[:, c : c + 1],
                         scale=1.0,
                     )
+                    if c == 1 and s in LN_BATCHES:
+                        guess(*LN_BATCHES[s])
+                    if c == 1 and s - 1 in LN_BATCHES:
+                        guess_again(*LN_BATCHES[s - 1])
+
+        def guess(lo, hi):
+            cols = slice(4 * lo, 4 * hi)
+            bits = ssum[:, cols].bitcast(U32)
+            nc.scalar.activation(out=lny[:, cols], in_=bits, func=ACT.Identity, bias=ebias[:], scale=-LN_SLOPE)
+            nc.scalar.activation(out=lne[:, cols], in_=bits, func=ACT.Exp, bias=ebias[:], scale=-LN_SLOPE)
+
+        def guess_again(lo, hi):
+            cols = slice(4 * lo, 4 * hi)
+            nc.scalar.activation(out=lne[:, cols], in_=lnb[:, cols], func=ACT.Exp, scale=1.0)
+
+        def ln_poly(lo, hi):
+            cols = slice(4 * lo, 4 * hi)
+            t, g, e = lnt[:, cols], lng[:, cols], lne[:, cols]
+            stt = nc.vector.scalar_tensor_tensor
+            return [
+                lambda: stt(out=t, in0=ssum[:, cols], scalar=-1.0 / CUBE3, in1=e, op0=ALU.mult, op1=ALU.mult),
+                lambda: stt(out=g, in0=t, scalar=1.5 * CUBE3 * CUBE3, in1=t, op0=ALU.add, op1=ALU.mult),
+                lambda: stt(out=g, in0=g, scalar=3.0 * CUBE3, in1=t, op0=ALU.add, op1=ALU.mult),
+            ]
+
+        def stage1(lo, hi):
+            cols = slice(4 * lo, 4 * hi)
+            return ln_poly(lo, hi) + [
+                lambda: nc.vector.scalar_tensor_tensor(
+                    out=lnb[:, cols], in0=lng[:, cols], scalar=11.0 / 6.0, in1=lny[:, cols], op0=ALU.add, op1=ALU.add
+                )
+            ]
+
+        def stage2(lo, hi):
+            cols = slice(4 * lo, 4 * hi)
+            p = ln_poly(lo, hi)
+            return [
+                p[0],
+                lambda: nc.vector.tensor_tensor(out=lny[:, cols], in0=lnb[:, cols], in1=negm[:, cols], op=ALU.add),
+                p[1],
+                p[2],
+            ]
+
+        def ln_last(b):
+            cols = slice(4 * b, 4 * (b + 1))
+            nc.vector.scalar_tensor_tensor(
+                out=negc_blocks[b][:], in0=lng[:, cols], scalar=11.0 / 6.0, in1=lny[:, cols], op0=ALU.add, op1=ALU.add
+            )
+
+        def finish_gp(b):
+            lt = ltiles[b]
+            for r in range(4):
+                nc.gpsimd.tensor_scalar(
+                    out=lt[:, r, :], in0=lt[:, r, :], scalar1=1.0, scalar2=negc_blocks[b][:, r : r + 1], op0=ALU.mult, op1=ALU.add
+                )
+            nc.sync.dma_start(out=out_rows[512 * b : 512 * (b + 1), :].rearrange("(r p) v -> p r v", p=P), in_=lt[:])
+
+        def finish_v(b):
+            lt = ltiles[b]
+            for q in range(2):
+                for r in (2 * q, 2 * q + 1):
+                    nc.vector.tensor_scalar(
+                        out=lt[:, r, :], in0=lt[:, r, :], scalar1=1.0, scalar2=negc_blocks[b][:, r : r + 1], op0=ALU.mult, op1=ALU.add
+                    )
+                base = 512 * b + 256 * q
+                nc.sync.dma_start(
+                    out=out_rows[base : base + 256, :].rearrange("(r p) v -> p r v", p=P), in_=lt[:, 2 * q : 2 * q + 2, :]
+                )
 
         def logits(b):
             xc, xs = xq[b]
@@ -264,9 +344,9 @@ def tile_joint_t_kernel(tc, h_pred, h_enc, W1, b1, W2, b2, out):
                         stop=(g == 1),
                     )
 
-        def exps(b):
+        def exps(b, tiles=range(4)):
             lt = ltiles[b]
-            for r in range(4):
+            for r in tiles:
                 i = 4 * b + r
                 junk = loop.tile([P, 512], BF16, tag="junk", bufs=2, name="junk%d" % i)
                 nc.scalar.activation(
@@ -278,12 +358,20 @@ def tile_joint_t_kernel(tc, h_pred, h_enc, W1, b1, W2, b2, out):
                     accum_out=ssum[:, i : i + 1],
                 )
 
+        def xg_tile(s, g):
+            xgs[(s, g)] = loop.tile([P, 512, 4], BF16, tag="xg", bufs=XG_BUFS, align_bytes=64, name="xg%d_%d" % (s, g))
+
+        def gp_regroup(s):
+            if 1 <= s < BLOCKS:
+                xg_tile(s, 0)
+                cols = slice(512 - GP_COLS, 512)
+                gp_copy(xgs[(s, 0)][:, cols, :], xps[(s, 0)][:, :, cols].rearrange("p t w -> p w t"))
+
         def v_regroup(s, g):
-            if s >= BLOCKS:
-                return
-            xg = loop.tile([P, 512, 4], BF16, tag="xg", bufs=2, align_bytes=64, name="xg%d_%d" % (s, g))
-            xgs[(s, g)] = xg
-            regroup(nc.vector.tensor_copy, xg[:], xps[(s, g)][:])
+            cols = slice(0, 512 - GP_COLS if g == 0 and s > 0 else 512)
+            if g == 1 or s == 0:
+                xg_tile(s, g)
+            regroup(nc.vector.tensor_copy, xgs[(s, g)][:, cols, :], xps[(s, g)][:, :, cols])
 
         def v_quant(s, g):
             if s >= BLOCKS:
@@ -315,89 +403,99 @@ def tile_joint_t_kernel(tc, h_pred, h_enc, W1, b1, W2, b2, out):
 
         def v_max_block(b):
             if b >= 0 and b not in FINE:
-                nc.vector.tensor_reduce(
-                    out=negm[:, 4 * b : 4 * (b + 1)], in_=ltiles[b][:], axis=AX.X, op=ALU.max, negate=True
-                )
+                for lo, hi in ((0, 3), (3, 4)):
+                    nc.vector.tensor_reduce(
+                        out=negm[:, 4 * b + lo : 4 * b + hi], in_=ltiles[b][:, lo:hi, :], axis=AX.X, op=ALU.max, negate=True
+                    )
 
-        batch_start = 0
-        for s in range(BLOCKS + 2):
+        def iter_steps(s):
+            steps = []
+            if s - 1 in LN_BATCHES:
+                steps.extend(stage2(*LN_BATCHES[s - 1]))
+            if s in LN_BATCHES:
+                steps.extend(stage1(*LN_BATCHES[s]))
+            return steps
+
+        def finish(s):
+            for bb in FINISH.get(s, ()):
+                ln_last(bb)
+                finish_gp(bb)
+
+        def run(steps):
+            if steps:
+                step = steps[0]
+                steps.remove(step)
+                step()
+
+        for s in range(BLOCKS + 1):
             if s < BLOCKS:
                 z_tanh(s)
+                gp_regroup(s)
             if s == 0:
                 regroup(nc.scalar.copy, w2g[0][:], w2raw[0][:])
-            if 1 <= s <= BLOCKS:
+            if s >= 1:
                 logits(s - 1)
+            if s == BLOCKS:
+                guess(*LN_BATCHES[s])
             if s >= 2:
                 exps(s - 2)
-            if s <= BLOCKS:
-                b = s - 1
+            b = s - 1
+            steps = iter_steps(s)
+            if s < BLOCKS:
                 v_regroup(s, 0)
+                run(steps)
                 v_regroup(s, 1)
+                run(steps)
                 v_quant(s, 0)
+                run(steps)
                 v_quant(s, 1)
-                v_bias(b, 0)
-                v_bias(b, 1)
-                v_max_tile(b, 0)
-                v_bias(b, 2)
-                v_max_tile(b, 1)
-                v_bias(b, 3)
-                v_max_tile(b, 2)
-                v_max_tile(b, 3)
-                v_max_block(b)
-                if s == 0:
-                    quant_he(1)
-                    for g in (1, 0):
-                        nc.vector.quantize_mx(
-                            out=w2c[:, g, :].bitcast(FP8X4),
-                            scales=w2s[:, g, :],
-                            in_=w2g[g][:].rearrange("p w t -> p (w t)"),
-                        )
-                if s == 1:
-                    quant_he(2)
-                if s == 2:
-                    quant_he(3)
-                moves(s + 2)
-            if s - 2 in LN_AFTER:
-                last = s - 2
-                lo, hi = 4 * batch_start, 4 * (last + 1)
-                nc.scalar.activation(out=lns[:, lo:hi], in_=ssum[:, lo:hi], func=ACT.Ln)
-                gp_blocks = [bb for bb in range(batch_start, last + 1) if bb not in ON_VECTOR]
-                if gp_blocks:
-                    glo, ghi = 4 * gp_blocks[0], 4 * (gp_blocks[-1] + 1)
-                    nc.gpsimd.tensor_tensor(
-                        out=negc[:, glo:ghi], in0=negm[:, glo:ghi], in1=lns[:, glo:ghi], op=ALU.subtract
+                run(steps)
+            if s - 1 not in LN_BATCHES:
+                finish(s)
+            v_bias(b, 0)
+            if s - 1 in LN_BATCHES:
+                finish(s)
+            run(steps)
+            v_bias(b, 1)
+            run(steps)
+            v_max_tile(b, 0)
+            run(steps)
+            v_bias(b, 2)
+            v_max_tile(b, 1)
+            run(steps)
+            v_bias(b, 3)
+            v_max_tile(b, 2)
+            v_max_tile(b, 3)
+            v_max_block(b)
+            if s == 0:
+                quant_he(1)
+                for g in (1, 0):
+                    nc.vector.quantize_mx(
+                        out=w2c[:, g, :].bitcast(FP8X4),
+                        scales=w2s[:, g, :],
+                        in_=w2g[g][:].rearrange("p w t -> p (w t)"),
                     )
-                for bb in range(batch_start, last + 1):
-                    lt = ltiles[bb]
-                    if bb not in ON_VECTOR:
-                        for r in range(4):
-                            i = 4 * bb + r
-                            nc.gpsimd.tensor_scalar(
-                                out=lt[:, r, :],
-                                in0=lt[:, r, :],
-                                scalar1=1.0,
-                                scalar2=negc[:, i : i + 1],
-                                op0=ALU.mult,
-                                op1=ALU.add,
-                            )
-                        nc.sync.dma_start(
-                            out=out_rows[512 * bb : 512 * (bb + 1), :].rearrange("(r p) v -> p r v", p=P), in_=lt[:]
-                        )
-                    else:
-                        for q in range(2):
-                            for r in (2 * q, 2 * q + 1):
-                                i = 4 * bb + r
-                                nc.vector.tensor_scalar(
-                                    out=lt[:, r, :],
-                                    in0=lt[:, r, :],
-                                    scalar1=negm[:, i : i + 1],
-                                    scalar2=lns[:, i : i + 1],
-                                    op0=ALU.add,
-                                    op1=ALU.subtract,
-                                )
-                            base = 512 * bb + 256 * q
-                            nc.sync.dma_start(
-                                out=out_rows[base : base + 256, :].rearrange("(r p) v -> p r v", p=P),
-                                in_=lt[:, 2 * q : 2 * q + 2, :],
-                            )
-                batch_start = last + 1
+            if s == 1:
+                quant_he(2)
+            if s == 2:
+                quant_he(3)
+            moves(s + 2)
+        guess(14, 15)
+        exps(15, (0,))
+        guess_again(12, 14)
+        exps(15, (1, 2))
+        for step in stage2(12, 14) + stage1(14, 15):
+            step()
+        guess_again(14, 15)
+        exps(15, (3,))
+        for bb in (12, 13):
+            ln_last(bb)
+            finish_v(bb)
+        for step in stage2(14, 15):
+            step()
+        ln_last(14)
+        finish_v(14)
+        cols = slice(60, 64)
+        nc.scalar.activation(out=lne[:, cols], in_=ssum[:, cols], func=ACT.Ln)
+        nc.vector.tensor_tensor(out=negc_blocks[15][:], in0=negm[:, cols], in1=lne[:, cols], op=ALU.subtract)
+        finish_v(15)

@@ -24,8 +24,7 @@ LN_BATCHES = {6: (0, 4), 10: (4, 8), 12: (8, 10), 14: (10, 12), 16: (12, 14)}
 FINISH = {7: (0,), 8: (1,), 9: (2,), 10: (3,), 11: (4,), 12: (5, 6), 13: (7, 8), 14: (9,), 15: (10, 11)}
 W1_PIECES = ((0, 256), (256, 256), (512, 256), (768, 256))
 HE_PIECES = ((0, 32), (32, 32), (64, 64), (128, 128))
-XG_BUFS = 3
-GP_COLS = 256
+ON_SCALAR = (0, 1, 2)
 FINE = (15,)
 
 
@@ -307,13 +306,19 @@ def tile_joint_t_kernel(tc, h_pred, h_enc, W1, b1, W2, b2, out):
                 out=negc_blocks[b][:], in0=lng[:, cols], scalar=11.0 / 6.0, in1=lny[:, cols], op0=ALU.add, op1=ALU.add
             )
 
-        def finish_gp(b):
+        def finish_on_scalar(b):
+            lt = ltiles[b]
+            for r in ON_SCALAR:
+                nc.scalar.activation(out=lt[:, r, :], in_=lt[:, r, :], func=ACT.Identity, bias=negc_blocks[b][:, r : r + 1], scale=1.0)
+            nc.sync.dma_start(out=out_rows[512 * b : 512 * (b + 1), :].rearrange("(r p) v -> p r v", p=P), in_=lt[:])
+
+        def finish_on_vector(b):
             lt = ltiles[b]
             for r in range(4):
-                nc.gpsimd.tensor_scalar(
-                    out=lt[:, r, :], in0=lt[:, r, :], scalar1=1.0, scalar2=negc_blocks[b][:, r : r + 1], op0=ALU.mult, op1=ALU.add
-                )
-            nc.sync.dma_start(out=out_rows[512 * b : 512 * (b + 1), :].rearrange("(r p) v -> p r v", p=P), in_=lt[:])
+                if r not in ON_SCALAR:
+                    nc.vector.tensor_scalar(
+                        out=lt[:, r, :], in0=lt[:, r, :], scalar1=1.0, scalar2=negc_blocks[b][:, r : r + 1], op0=ALU.mult, op1=ALU.add
+                    )
 
         def finish_v(b):
             lt = ltiles[b]
@@ -359,19 +364,11 @@ def tile_joint_t_kernel(tc, h_pred, h_enc, W1, b1, W2, b2, out):
                 )
 
         def xg_tile(s, g):
-            xgs[(s, g)] = loop.tile([P, 512, 4], BF16, tag="xg", bufs=XG_BUFS, align_bytes=64, name="xg%d_%d" % (s, g))
-
-        def gp_regroup(s):
-            if 1 <= s < BLOCKS:
-                xg_tile(s, 0)
-                cols = slice(512 - GP_COLS, 512)
-                gp_copy(xgs[(s, 0)][:, cols, :], xps[(s, 0)][:, :, cols].rearrange("p t w -> p w t"))
+            xgs[(s, g)] = loop.tile([P, 512, 4], BF16, tag="xg", bufs=2, align_bytes=64, name="xg%d_%d" % (s, g))
 
         def v_regroup(s, g):
-            cols = slice(0, 512 - GP_COLS if g == 0 and s > 0 else 512)
-            if g == 1 or s == 0:
-                xg_tile(s, g)
-            regroup(nc.vector.tensor_copy, xgs[(s, g)][:, cols, :], xps[(s, g)][:, :, cols])
+            xg_tile(s, g)
+            regroup(nc.vector.tensor_copy, xgs[(s, g)][:], xps[(s, g)][:])
 
         def v_quant(s, g):
             if s >= BLOCKS:
@@ -419,7 +416,10 @@ def tile_joint_t_kernel(tc, h_pred, h_enc, W1, b1, W2, b2, out):
         def finish(s):
             for bb in FINISH.get(s, ()):
                 ln_last(bb)
-                finish_gp(bb)
+
+        def finish_tiles(s):
+            for bb in FINISH.get(s, ()):
+                finish_on_vector(bb)
 
         def run(steps):
             if steps:
@@ -430,11 +430,12 @@ def tile_joint_t_kernel(tc, h_pred, h_enc, W1, b1, W2, b2, out):
         for s in range(BLOCKS + 1):
             if s < BLOCKS:
                 z_tanh(s)
-                gp_regroup(s)
             if s == 0:
                 regroup(nc.scalar.copy, w2g[0][:], w2raw[0][:])
             if s >= 1:
                 logits(s - 1)
+            for bb in FINISH.get(s - 1, ()):
+                finish_on_scalar(bb)
             if s == BLOCKS:
                 guess(*LN_BATCHES[s])
             if s >= 2:
@@ -467,6 +468,7 @@ def tile_joint_t_kernel(tc, h_pred, h_enc, W1, b1, W2, b2, out):
             v_max_tile(b, 2)
             v_max_tile(b, 3)
             v_max_block(b)
+            finish_tiles(s)
             if s == 0:
                 quant_he(1)
                 for g in (1, 0):

@@ -20,11 +20,8 @@ BLOCKS = 16
 LN_SLOPE = 355.0 / 512.0 / 2.0**23
 LN_OFFSET = -127.0 * 355.0 / 512.0 + 61.0 / 2048.0
 CUBE3 = 3.0 ** (1.0 / 3.0)
-LN_BATCHES = {6: (0, 4), 10: (4, 8), 12: (8, 10), 14: (10, 12), 16: (12, 14)}
-FINISH = {7: (0,), 8: (1,), 9: (2,), 10: (3,), 11: (4,), 12: (5, 6), 13: (7, 8), 14: (9,), 15: (10, 11)}
 W1_PIECES = ((0, 256), (256, 256), (512, 256), (768, 256))
 HE_PIECES = ((0, 32), (32, 32), (64, 64), (128, 128))
-ON_SCALAR = (0, 1, 2)
 FINE = (15,)
 
 
@@ -257,10 +254,11 @@ def tile_joint_t_kernel(tc, h_pred, h_enc, W1, b1, W2, b2, out):
                         bias=b1_sb[:, c : c + 1],
                         scale=1.0,
                     )
-                    if c == 1 and s in LN_BATCHES:
-                        guess(*LN_BATCHES[s])
-                    if c == 1 and s - 1 in LN_BATCHES:
-                        guess_again(*LN_BATCHES[s - 1])
+                    if c == 1 and s >= 4:
+                        if s % 2 == 0:
+                            guess(s - 4, s - 2)
+                        else:
+                            guess_again(s - 5, s - 3)
 
         def guess(lo, hi):
             cols = slice(4 * lo, 4 * hi)
@@ -306,19 +304,13 @@ def tile_joint_t_kernel(tc, h_pred, h_enc, W1, b1, W2, b2, out):
                 out=negc_blocks[b][:], in0=lng[:, cols], scalar=11.0 / 6.0, in1=lny[:, cols], op0=ALU.add, op1=ALU.add
             )
 
-        def finish_on_scalar(b):
-            lt = ltiles[b]
-            for r in ON_SCALAR:
-                nc.scalar.activation(out=lt[:, r, :], in_=lt[:, r, :], func=ACT.Identity, bias=negc_blocks[b][:, r : r + 1], scale=1.0)
-            nc.sync.dma_start(out=out_rows[512 * b : 512 * (b + 1), :].rearrange("(r p) v -> p r v", p=P), in_=lt[:])
-
-        def finish_on_vector(b):
+        def finish_gp(b):
             lt = ltiles[b]
             for r in range(4):
-                if r not in ON_SCALAR:
-                    nc.vector.tensor_scalar(
-                        out=lt[:, r, :], in0=lt[:, r, :], scalar1=1.0, scalar2=negc_blocks[b][:, r : r + 1], op0=ALU.mult, op1=ALU.add
-                    )
+                nc.gpsimd.tensor_scalar(
+                    out=lt[:, r, :], in0=lt[:, r, :], scalar1=1.0, scalar2=negc_blocks[b][:, r : r + 1], op0=ALU.mult, op1=ALU.add
+                )
+            nc.sync.dma_start(out=out_rows[512 * b : 512 * (b + 1), :].rearrange("(r p) v -> p r v", p=P), in_=lt[:])
 
         def finish_v(b):
             lt = ltiles[b]
@@ -389,7 +381,7 @@ def tile_joint_t_kernel(tc, h_pred, h_enc, W1, b1, W2, b2, out):
                 return
             if r == 0:
                 ltiles[b] = lpool.tile([P, 4, 512], F32, tag="L", name="L%d" % b)
-            nc.vector.tensor_tensor(out=ltiles[b][:, r, :], in0=accs[(b, r)][:], in1=b2f[:], op=ALU.add)
+            nc.vector.tensor_tensor(out=ltiles[b][:, r, :], in0=b2f[:], in1=accs[(b, r)][:], op=ALU.add)
 
         def v_max_tile(b, r):
             if b in FINE:
@@ -406,20 +398,9 @@ def tile_joint_t_kernel(tc, h_pred, h_enc, W1, b1, W2, b2, out):
                     )
 
         def iter_steps(s):
-            steps = []
-            if s - 1 in LN_BATCHES:
-                steps.extend(stage2(*LN_BATCHES[s - 1]))
-            if s in LN_BATCHES:
-                steps.extend(stage1(*LN_BATCHES[s]))
-            return steps
-
-        def finish(s):
-            for bb in FINISH.get(s, ()):
-                ln_last(bb)
-
-        def finish_tiles(s):
-            for bb in FINISH.get(s, ()):
-                finish_on_vector(bb)
+            if s < 4:
+                return []
+            return stage1(s - 4, s - 2) if s % 2 == 0 else stage2(s - 5, s - 3)
 
         def run(steps):
             if steps:
@@ -434,10 +415,8 @@ def tile_joint_t_kernel(tc, h_pred, h_enc, W1, b1, W2, b2, out):
                 regroup(nc.scalar.copy, w2g[0][:], w2raw[0][:])
             if s >= 1:
                 logits(s - 1)
-            for bb in FINISH.get(s - 1, ()):
-                finish_on_scalar(bb)
             if s == BLOCKS:
-                guess(*LN_BATCHES[s])
+                guess(12, 14)
             if s >= 2:
                 exps(s - 2)
             b = s - 1
@@ -451,11 +430,7 @@ def tile_joint_t_kernel(tc, h_pred, h_enc, W1, b1, W2, b2, out):
                 run(steps)
                 v_quant(s, 1)
                 run(steps)
-            if s - 1 not in LN_BATCHES:
-                finish(s)
             v_bias(b, 0)
-            if s - 1 in LN_BATCHES:
-                finish(s)
             run(steps)
             v_bias(b, 1)
             run(steps)
@@ -467,8 +442,10 @@ def tile_joint_t_kernel(tc, h_pred, h_enc, W1, b1, W2, b2, out):
             v_bias(b, 3)
             v_max_tile(b, 2)
             v_max_tile(b, 3)
+            if s >= 5:
+                ln_last(s - 5)
+                finish_gp(s - 5)
             v_max_block(b)
-            finish_tiles(s)
             if s == 0:
                 quant_he(1)
                 for g in (1, 0):

@@ -20,8 +20,9 @@ BLOCKS = 16
 LN_SLOPE = 355.0 / 512.0 / 2.0**23
 LN_OFFSET = -127.0 * 355.0 / 512.0 + 61.0 / 2048.0
 CUBE3 = 3.0 ** (1.0 / 3.0)
-W1_PIECES = ((0, 256), (256, 256), (512, 256), (768, 256))
-HE_PIECES = ((0, 32), (32, 32), (64, 64), (128, 128))
+W1_PIECES = ((0, 128), (128, 128), (256, 256), (512, 256), (768, 256))
+HE_PIECES = ((0, 16), (16, 16), (32, 32), (64, 64), (128, 64), (192, 64))
+SHARE = 160
 FINE = (15,)
 
 
@@ -50,13 +51,10 @@ def tile_joint_t_kernel(tc, h_pred, h_enc, W1, b1, W2, b2, out):
         he8_s = const.tile([P, 2048], U8, align_bytes=64)
         nc.vector.memset(hp_s[:].bitcast(I32), 0)
 
-        he_sb = prep.tile([P, 2, 512], BF16)
-        nc.sync.dma_start(out=he_sb[:], in_=h_enc.flatten_outer_dims().rearrange("(a p) k -> p a k", p=P))
-        hp_sb = prep.tile([P, 512], BF16)
-        nc.sync.dma_start(out=hp_sb[:], in_=h_pred.flatten_outer_dims())
-        nc.sync.dma_start(out=b1t[0:8, :], in_=b1.rearrange("(c p) -> c p", p=P))
         w1raw = {}
-        for h, (j0, jw) in enumerate(W1_PIECES):
+
+        def load_w1(h):
+            j0, jw = W1_PIECES[h]
             for g in range(2):
                 raw = prep.tile([P, 4, jw], BF16, name="w1raw%d%d" % (g, h))
                 nc.sync.dma_start(
@@ -64,6 +62,19 @@ def tile_joint_t_kernel(tc, h_pred, h_enc, W1, b1, W2, b2, out):
                     in_=W1[512 * g : 512 * (g + 1), j0 : j0 + jw].rearrange("(t p) j -> p t j", p=P),
                 )
                 w1raw[(g, h)] = raw
+
+        he_sb = prep.tile([P, 2, 512], BF16)
+        he_rows = h_enc.flatten_outer_dims().rearrange("(a p) k -> p a k", p=P)
+        hp_sb = prep.tile([P, 512], BF16)
+        nc.sync.dma_start(out=he_sb[:, 0, :], in_=he_rows[:, 0, :])
+        load_w1(0)
+        nc.sync.dma_start(out=hp_sb[:], in_=h_pred.flatten_outer_dims())
+        nc.sync.dma_start(out=b1t[0:8, :], in_=b1.rearrange("(c p) -> c p", p=P))
+        load_w1(1)
+        nc.sync.dma_start(out=he_sb[:, 1, :], in_=he_rows[:, 1, :])
+        load_w1(2)
+        load_w1(3)
+        load_w1(4)
         w2raw = {}
         for g in range(2):
             raw = prep.tile([P, 4, 512], BF16, tag="w2raw", bufs=2, name="w2raw%d" % g)
@@ -84,7 +95,6 @@ def tile_joint_t_kernel(tc, h_pred, h_enc, W1, b1, W2, b2, out):
         hp_c = const.tile([P, 128], U32, align_bytes=64)
         he8_c = const.tile([P, 2048], U32, align_bytes=64)
         b1_sb = const.tile([P, 8], F32)
-        b2f = const.tile([P, 512], F32)
         negm = const.tile([P, 64], F32)
         ssum = const.tile([P, 64], F32)
         lny = const.tile([P, 64], F32)
@@ -112,14 +122,15 @@ def tile_joint_t_kernel(tc, h_pred, h_enc, W1, b1, W2, b2, out):
             for t in range(4):
                 nc.tensor.transpose(hpT[:, t, :], hp_sb[:, P * t : P * (t + 1)], ident[:])
             nc.tensor.transpose(b1T[:], b1t[:], ident[:])
-            for t in range(4):
-                nc.tensor.transpose(heT[:, 1, t, :], he_sb[:, 1, P * t : P * (t + 1)], ident[:])
             nc.scalar.copy(out=he_lin[:, 0], in_=heT[:, 0])
             nc.scalar.copy(out=hp_g[:], in_=hpT[:].rearrange("p t r -> p r t"))
             nc.scalar.copy(out=b1_sb[:], in_=b1T[:, 0:8])
-            regroup(nc.scalar.copy, w1g[(1, 0)][:], w1raw[(1, 0)][:])
-            nc.scalar.copy(out=he_lin[:, 1], in_=heT[:, 1])
             regroup(nc.scalar.copy, w1g[(1, 1)][:], w1raw[(1, 1)][:])
+            for t in range(4):
+                nc.tensor.transpose(heT[:, 1, t, :], he_sb[:, 1, P * t : P * (t + 1)], ident[:])
+            nc.scalar.copy(out=he_lin[:, 1], in_=heT[:, 1])
+            regroup(nc.scalar.copy, w1g[(1, 2)][:], w1raw[(1, 2)][:])
+            regroup(nc.scalar.copy, w1g[(1, 3)][:], w1raw[(1, 3)][:])
 
         def he_views(piece):
             r0, nr = HE_PIECES[piece]
@@ -129,9 +140,6 @@ def tile_joint_t_kernel(tc, h_pred, h_enc, W1, b1, W2, b2, out):
                 he_lin[:, a, :, q0 : q0 + nr].rearrange("p t r -> p r t").unsqueeze(2).to_broadcast([P, nr, 8, 4])
             )
             return dst, src
-
-        def gp_copy(dst, src):
-            nc.gpsimd.tensor_scalar(out=dst, in0=src, scalar1=1.0, scalar2=0.0, op0=ALU.mult, op1=ALU.add)
 
         def quant_he(piece):
             r0, nr = HE_PIECES[piece]
@@ -175,37 +183,64 @@ def tile_joint_t_kernel(tc, h_pred, h_enc, W1, b1, W2, b2, out):
                 in_=w1g[(g, h)][:].rearrange("p w t -> p (w t)"),
             )
 
-        dst, src = he_views(0)
-        nc.vector.tensor_copy(out=dst, in_=src)
-        regroup(nc.vector.tensor_copy, w1g[(0, 0)][:], w1raw[(0, 0)][:])
-        quant_he(0)
-        nc.vector.quantize_mx(
-            out=hp_c[:].bitcast(FP8X4), scales=hp_s[:], in_=hp_g[:].rearrange("p r t -> p (r t)")
-        )
-        quant_w1(0, 0)
-        moves(0)
-        quant_w1(1, 0)
-        regroup(nc.vector.tensor_copy, w1g[(0, 1)][:], w1raw[(0, 1)][:])
-        gp_copy(w1g[(1, 2)][:], w1raw[(1, 2)][:].rearrange("p t w -> p w t"))
-        gp_copy(w1g[(1, 3)][:], w1raw[(1, 3)][:].rearrange("p t w -> p w t"))
-        dst, src = he_views(1)
-        gp_copy(dst, src)
+        def v_he(piece):
+            dst, src = he_views(piece)
+            nc.vector.tensor_copy(out=dst, in_=src)
+            quant_he(piece)
+
+        def hand_over(piece):
+            r0, nr = HE_PIECES[piece]
+            a, q0 = r0 // P, r0 % P
+            hand = prep.tile([P, 4, 64], BF16, tag="hand", bufs=2, name="hand%d" % piece)
+            nc.vector.tensor_copy(out=hand[:, :, :nr], in_=he_lin[:, a, :, q0 : q0 + nr])
+            nc.gpsimd.tensor_scalar(
+                out=he_g[:, r0 : r0 + nr, :, :],
+                in0=hand[:, :, :nr].rearrange("p t r -> p r t").unsqueeze(2).to_broadcast([P, nr, 8, 4]),
+                scalar1=1.0,
+                scalar2=0.0,
+                op0=ALU.mult,
+                op1=ALU.add,
+            )
+
+        def quant_w2(g):
+            nc.vector.quantize_mx(
+                out=w2c[:, g, :].bitcast(FP8X4),
+                scales=w2s[:, g, :],
+                in_=w2g[g][:].rearrange("p w t -> p (w t)"),
+            )
+
+        def v_w1(g, h):
+            regroup(nc.vector.tensor_copy, w1g[(g, h)][:], w1raw[(g, h)][:])
+
         w2g = {}
         for g in range(2):
             w2g[g] = prep.tile([P, 512, 4], BF16, tag="w2g", bufs=2, align_bytes=64, name="w2g%d" % g)
-        gp_copy(w2g[1][:], w2raw[1][:].rearrange("p t w -> p w t"))
-        gp_copy(b2f[:], b2b[:])
-        for piece in (2, 3):
-            dst, src = he_views(piece)
-            gp_copy(dst, src)
+
+        v_w1(0, 0)
+        v_w1(1, 0)
+        quant_w1(0, 0)
+        quant_w1(1, 0)
+        dst, src = he_views(0)
+        nc.vector.tensor_copy(out=dst, in_=src)
+        nc.vector.quantize_mx(
+            out=hp_c[:].bitcast(FP8X4), scales=hp_s[:], in_=hp_g[:].rearrange("p r t -> p (r t)")
+        )
+        quant_he(0)
+        moves(0)
+        v_w1(0, 1)
+        v_w1(0, 2)
         quant_w1(0, 1)
         quant_w1(1, 1)
-        regroup(nc.vector.tensor_copy, w1g[(0, 2)][:], w1raw[(0, 2)][:])
-        regroup(nc.vector.tensor_copy, w1g[(0, 3)][:], w1raw[(0, 3)][:])
+        v_w1(0, 3)
         quant_w1(0, 2)
         quant_w1(1, 2)
+        v_w1(0, 4)
+        v_w1(1, 4)
         quant_w1(0, 3)
         quant_w1(1, 3)
+        quant_w1(0, 4)
+        quant_w1(1, 4)
+        v_he(1)
 
         zps = ctx.enter_context(tc.psum_pool(name="zps", bufs=4))
         lps = ctx.enter_context(tc.psum_pool(name="lps", bufs=4))
@@ -304,13 +339,50 @@ def tile_joint_t_kernel(tc, h_pred, h_enc, W1, b1, W2, b2, out):
                 out=negc_blocks[b][:], in0=lng[:, cols], scalar=11.0 / 6.0, in1=lny[:, cols], op0=ALU.add, op1=ALU.add
             )
 
-        def finish_gp(b):
+        def sub_g(b, r):
             lt = ltiles[b]
+            nc.gpsimd.tensor_scalar(
+                out=lt[:, r, :], in0=lt[:, r, :], scalar1=1.0, scalar2=negc_blocks[b][:, r : r + 1], op0=ALU.mult, op1=ALU.add
+            )
+
+        def store(b):
+            nc.sync.dma_start(out=out_rows[512 * b : 512 * (b + 1), :].rearrange("(r p) v -> p r v", p=P), in_=ltiles[b][:])
+
+        def finish_gp(b):
             for r in range(4):
-                nc.gpsimd.tensor_scalar(
-                    out=lt[:, r, :], in0=lt[:, r, :], scalar1=1.0, scalar2=negc_blocks[b][:, r : r + 1], op0=ALU.mult, op1=ALU.add
-                )
-            nc.sync.dma_start(out=out_rows[512 * b : 512 * (b + 1), :].rearrange("(r p) v -> p r v", p=P), in_=lt[:])
+                sub_g(b, r)
+            store(b)
+
+        def sub_s(b, r):
+            lt = ltiles[b]
+            nc.scalar.activation(
+                out=lt[:, r, :], in_=lt[:, r, :], func=ACT.Identity, bias=negc_blocks[b][:, r : r + 1], scale=1.0
+            )
+
+        def sub_v(b, r):
+            lt = ltiles[b]
+            nc.vector.tensor_scalar(
+                out=lt[:, r, :], in0=lt[:, r, :], scalar1=1.0, scalar2=negc_blocks[b][:, r : r + 1], op0=ALU.mult, op1=ALU.add
+            )
+
+        def store_half(b, q):
+            base = 512 * b + 256 * q
+            nc.sync.dma_start(
+                out=out_rows[base : base + 256, :].rearrange("(r p) v -> p r v", p=P), in_=ltiles[b][:, 2 * q : 2 * q + 2, :]
+            )
+
+        def finish_s(b):
+            for r in range(4):
+                sub_s(b, r)
+            store(b)
+
+        def finish_both(b):
+            for r in (2, 3):
+                sub_s(b, r)
+            for r in (0, 1):
+                sub_v(b, r)
+            store_half(b, 0)
+            store_half(b, 1)
 
         def finish_v(b):
             lt = ltiles[b]
@@ -359,8 +431,19 @@ def tile_joint_t_kernel(tc, h_pred, h_enc, W1, b1, W2, b2, out):
             xgs[(s, g)] = loop.tile([P, 512, 4], BF16, tag="xg", bufs=2, align_bytes=64, name="xg%d_%d" % (s, g))
 
         def v_regroup(s, g):
-            xg_tile(s, g)
-            regroup(nc.vector.tensor_copy, xgs[(s, g)][:], xps[(s, g)][:])
+            if g == 0:
+                xg_tile(s, 0)
+            lo = share(s) if g == 1 else 0
+            regroup(nc.vector.tensor_copy, xgs[(s, g)][:, lo:, :], xps[(s, g)][:, :, lo:])
+
+        def share(s):
+            return SHARE if s >= 1 else 0
+
+        def s_regroup(s):
+            xg_tile(s, 1)
+            hi = share(s)
+            if hi:
+                regroup(nc.scalar.copy, xgs[(s, 1)][:, :hi, :], xps[(s, 1)][:, :, :hi])
 
         def v_quant(s, g):
             if s >= BLOCKS:
@@ -381,17 +464,16 @@ def tile_joint_t_kernel(tc, h_pred, h_enc, W1, b1, W2, b2, out):
                 return
             if r == 0:
                 ltiles[b] = lpool.tile([P, 4, 512], F32, tag="L", name="L%d" % b)
-            nc.vector.tensor_tensor(out=ltiles[b][:, r, :], in0=b2f[:], in1=accs[(b, r)][:], op=ALU.add)
+            nc.vector.tensor_tensor(out=ltiles[b][:, r, :], in0=b2b[:], in1=accs[(b, r)][:], op=ALU.add)
 
         def v_max_tile(b, r):
-            if b in FINE:
-                i = 4 * b + r
-                nc.vector.tensor_reduce(
-                    out=negm[:, i : i + 1], in_=ltiles[b][:, r, :], axis=AX.X, op=ALU.max, negate=True
-                )
+            i = 4 * b + r
+            nc.vector.tensor_reduce(
+                out=negm[:, i : i + 1], in_=ltiles[b][:, r, :], axis=AX.X, op=ALU.max, negate=True
+            )
 
         def v_max_block(b):
-            if b >= 0 and b not in FINE:
+            if b >= 0:
                 for lo, hi in ((0, 3), (3, 4)):
                     nc.vector.tensor_reduce(
                         out=negm[:, 4 * b + lo : 4 * b + hi], in_=ltiles[b][:, lo:hi, :], axis=AX.X, op=ALU.max, negate=True
@@ -408,15 +490,11 @@ def tile_joint_t_kernel(tc, h_pred, h_enc, W1, b1, W2, b2, out):
                 steps.remove(step)
                 step()
 
-        for s in range(BLOCKS + 1):
-            if s < BLOCKS:
-                z_tanh(s)
-            if s == 0:
+        for s in range(BLOCKS):
+            z_tanh(s)
+            if s == 1:
                 regroup(nc.scalar.copy, w2g[0][:], w2raw[0][:])
-            if s >= 1:
-                logits(s - 1)
-            if s == BLOCKS:
-                guess(12, 14)
+            s_regroup(s)
             if s >= 2:
                 exps(s - 2)
             b = s - 1
@@ -430,46 +508,70 @@ def tile_joint_t_kernel(tc, h_pred, h_enc, W1, b1, W2, b2, out):
                 run(steps)
                 v_quant(s, 1)
                 run(steps)
-            v_bias(b, 0)
-            run(steps)
-            v_bias(b, 1)
-            run(steps)
-            v_max_tile(b, 0)
-            run(steps)
-            v_bias(b, 2)
-            v_max_tile(b, 1)
-            run(steps)
-            v_bias(b, 3)
-            v_max_tile(b, 2)
-            v_max_tile(b, 3)
-            if s >= 5:
-                ln_last(s - 5)
-                finish_gp(s - 5)
+            if s == 1:
+                quant_w2(0)
+            if 3 <= s <= 5:
+                quant_he(s)
+            if s >= 1:
+                logits(b)
+            if 2 <= s <= 4:
+                hand_over(s + 1)
+            if s == BLOCKS - 1:
+                break
+            for r in range(4):
+                if r == 3 and s >= 5:
+                    ln_last(s - 5)
+                    finish_gp(s - 5)
+                v_bias(b, r)
+                run(steps)
             v_max_block(b)
             if s == 0:
-                quant_he(1)
-                for g in (1, 0):
-                    nc.vector.quantize_mx(
-                        out=w2c[:, g, :].bitcast(FP8X4),
-                        scales=w2s[:, g, :],
-                        in_=w2g[g][:].rearrange("p w t -> p (w t)"),
-                    )
-            if s == 1:
-                quant_he(2)
-            if s == 2:
-                quant_he(3)
+                regroup(nc.vector.tensor_copy, w2g[1][:], w2raw[1][:])
+                quant_w2(1)
+                v_he(2)
             moves(s + 2)
-        guess(14, 15)
-        exps(15, (0,))
+        guess(12, 14)
+        steps = stage1(12, 14)
+        for bb in (10, 11):
+            ln_last(bb)
+        finish_s(10)
+        for r in range(4):
+            v_bias(14, r)
+            run(steps)
         guess_again(12, 14)
+        finish_s(11)
+        steps = stage2(12, 14)
+        for r in range(4):
+            v_max_tile(14, r)
+            run(steps)
+        logits(15)
+        v_bias(15, 0)
+        ln_last(12)
+        ln_last(13)
+        finish_gp(12)
+        for r in (2, 3):
+            sub_g(13, r)
+        exps(14)
+        guess(14, 15)
+        sub_s(13, 0)
+        v_bias(15, 1)
+        v_max_tile(15, 0)
+        v_bias(15, 2)
+        v_max_tile(15, 1)
+        v_bias(15, 3)
+        steps = stage1(14, 15)
+        run(steps)
+        v_max_tile(15, 2)
+        run(steps)
+        v_max_tile(15, 3)
+        run(steps)
+        run(steps)
+        exps(15, (0,))
+        sub_s(13, 1)
+        store(13)
         exps(15, (1, 2))
-        for step in stage2(12, 14) + stage1(14, 15):
-            step()
         guess_again(14, 15)
         exps(15, (3,))
-        for bb in (12, 13):
-            ln_last(bb)
-            finish_v(bb)
         for step in stage2(14, 15):
             step()
         ln_last(14)
@@ -477,4 +579,4 @@ def tile_joint_t_kernel(tc, h_pred, h_enc, W1, b1, W2, b2, out):
         cols = slice(60, 64)
         nc.scalar.activation(out=lne[:, cols], in_=ssum[:, cols], func=ACT.Ln)
         nc.vector.tensor_tensor(out=negc_blocks[15][:], in0=negm[:, cols], in1=lne[:, cols], op=ALU.subtract)
-        finish_v(15)
+        finish_both(15)

@@ -22,7 +22,10 @@ LN_OFFSET = -127.0 * 355.0 / 512.0 + 61.0 / 2048.0
 CUBE3 = 3.0 ** (1.0 / 3.0)
 W1_PIECES = ((0, 128), (128, 128), (256, 256), (512, 256), (768, 256))
 HE_PIECES = ((0, 16), (16, 16), (32, 32), (64, 64), (128, 64), (192, 64))
-SHARE = 160
+GSHARE = 256
+GFIRST = 2
+SUB_AT = 0
+SHARE = 112
 FINE = (15,)
 
 
@@ -251,15 +254,16 @@ def tile_joint_t_kernel(tc, h_pred, h_enc, W1, b1, W2, b2, out):
         accs = {}
         ltiles = {}
 
-        def z_tanh(s):
-            pf_c, pf_s = pf[s // 4]
-
-            enc = slice(P * s, P * (s + 1))
-            for g in range(2):
-                xp = loop.tile([P, 4, 512], BF16, tag="xp", bufs=4, name="xp%d_%d" % (s, g))
-                xps[(s, g)] = xp
-                for tq in range(4):
-                    c = 4 * g + tq
+        def z_tanh(s, c):
+                if s >= BLOCKS:
+                    return
+                pf_c, pf_s = pf[s // 4]
+                enc = slice(P * s, P * (s + 1))
+                g, tq = c // 4, c % 4
+                if tq == 0:
+                    xps[(s, g)] = loop.tile([P, 4, 512], BF16, tag="xp", bufs=4, name="xp%d_%d" % (s, g))
+                xp = xps[(s, g)]
+                if True:
                     cols = slice(P * c, P * (c + 1))
                     zt = zps.tile([P, 512], F32, tag="z", name="z%d_%d" % (s, c))
                     for a in range(4):
@@ -289,11 +293,6 @@ def tile_joint_t_kernel(tc, h_pred, h_enc, W1, b1, W2, b2, out):
                         bias=b1_sb[:, c : c + 1],
                         scale=1.0,
                     )
-                    if c == 1 and s >= 4:
-                        if s % 2 == 0:
-                            guess(s - 4, s - 2)
-                        else:
-                            guess_again(s - 5, s - 3)
 
         def guess(lo, hi):
             cols = slice(4 * lo, 4 * hi)
@@ -396,9 +395,9 @@ def tile_joint_t_kernel(tc, h_pred, h_enc, W1, b1, W2, b2, out):
                     out=out_rows[base : base + 256, :].rearrange("(r p) v -> p r v", p=P), in_=lt[:, 2 * q : 2 * q + 2, :]
                 )
 
-        def logits(b):
+        def logits(b, r):
             xc, xs = xq[b]
-            for r in range(4):
+            if True:
                 rows = slice(P * r, P * (r + 1))
                 acc = lps.tile([P, 512], F32, tag="lg", name="lg%d_%d" % (b, r))
                 accs[(b, r)] = acc
@@ -428,18 +427,37 @@ def tile_joint_t_kernel(tc, h_pred, h_enc, W1, b1, W2, b2, out):
                 )
 
         def xg_tile(s, g):
-            xgs[(s, g)] = loop.tile([P, 512, 4], BF16, tag="xg", bufs=2, align_bytes=64, name="xg%d_%d" % (s, g))
+            xgs[(s, g)] = loop.tile([P, 512, 4], BF16, tag="xg%d" % g, bufs=2, align_bytes=64, name="xg%d_%d" % (s, g))
 
         def v_regroup(s, g):
-            if g == 0:
+            if g == 0 and (s, 0) not in xgs:
                 xg_tile(s, 0)
-            lo = share(s) if g == 1 else 0
+            lo = share(s) if g == 1 else gshare(s)
             regroup(nc.vector.tensor_copy, xgs[(s, g)][:, lo:, :], xps[(s, g)][:, :, lo:])
+
+        def g_regroup(s):
+            hi = gshare(s)
+            if hi:
+                xg_tile(s, 0)
+                dst, src = xgs[(s, 0)][:, :hi, :], xps[(s, 0)][:, :, :hi]
+                nc.gpsimd.tensor_scalar(
+                    out=dst.rearrange("p (c i) t -> p c t i", i=4),
+                    in0=src.rearrange("p t (c i) -> p c t i", i=4),
+                    scalar1=1.0,
+                    scalar2=0.0,
+                    op0=ALU.mult,
+                    op1=ALU.add,
+                )
+
+        def gshare(s):
+            return GSHARE if s >= GFIRST else 0
 
         def share(s):
             return SHARE if s >= 1 else 0
 
         def s_regroup(s):
+            if s >= BLOCKS:
+                return
             xg_tile(s, 1)
             hi = share(s)
             if hi:
@@ -490,46 +508,55 @@ def tile_joint_t_kernel(tc, h_pred, h_enc, W1, b1, W2, b2, out):
                 steps.remove(step)
                 step()
 
-        for s in range(BLOCKS):
-            z_tanh(s)
-            if s == 1:
-                regroup(nc.scalar.copy, w2g[0][:], w2raw[0][:])
+        for s in range(2):
+            for c in range(8):
+                z_tanh(s, c)
             s_regroup(s)
+        for s in range(BLOCKS):
+            if s >= 1:
+                for c in range(4, 8):
+                    z_tanh(s + 1, c)
+                s_regroup(s + 1)
             if s >= 2:
                 exps(s - 2)
+            if s >= 3 and s % 2 == 1 and s < 15:
+                guess(s - 3, s - 1)
             b = s - 1
             steps = iter_steps(s)
-            if s < BLOCKS:
-                v_regroup(s, 0)
-                run(steps)
-                v_regroup(s, 1)
-                run(steps)
-                v_quant(s, 0)
-                run(steps)
-                v_quant(s, 1)
-                run(steps)
-            if s == 1:
+            v_regroup(s, 0)
+            run(steps)
+            v_regroup(s, 1)
+            run(steps)
+            v_quant(s, 0)
+            run(steps)
+            v_quant(s, 1)
+            run(steps)
+            if s == 0:
+                v_he(2)
+                for g in range(2):
+                    regroup(nc.vector.tensor_copy, w2g[g][:], w2raw[g][:])
                 quant_w2(0)
-            if 3 <= s <= 5:
-                quant_he(s)
-            if s >= 1:
-                logits(b)
+                quant_w2(1)
             if 2 <= s <= 4:
-                hand_over(s + 1)
+                quant_he(s + 1)
             if s == BLOCKS - 1:
                 break
+            if 1 <= s <= 3:
+                hand_over(s + 2)
             for r in range(4):
-                if r == 3 and s >= 5:
+                if r == SUB_AT and s >= 5:
                     ln_last(s - 5)
                     finish_gp(s - 5)
+                if r == 0:
+                    g_regroup(s + 1)
                 v_bias(b, r)
+                logits(s, r)
+                z_tanh(s + 2, r)
+                if r == 0 and s >= 4 and s % 2 == 0:
+                    guess_again(s - 4, s - 2)
                 run(steps)
             v_max_block(b)
-            if s == 0:
-                regroup(nc.vector.tensor_copy, w2g[1][:], w2raw[1][:])
-                quant_w2(1)
-                v_he(2)
-            moves(s + 2)
+            moves(s + 3)
         guess(12, 14)
         steps = stage1(12, 14)
         for bb in (10, 11):
@@ -537,6 +564,7 @@ def tile_joint_t_kernel(tc, h_pred, h_enc, W1, b1, W2, b2, out):
         finish_s(10)
         for r in range(4):
             v_bias(14, r)
+            logits(15, r)
             run(steps)
         guess_again(12, 14)
         finish_s(11)
@@ -544,7 +572,6 @@ def tile_joint_t_kernel(tc, h_pred, h_enc, W1, b1, W2, b2, out):
         for r in range(4):
             v_max_tile(14, r)
             run(steps)
-        logits(15)
         v_bias(15, 0)
         ln_last(12)
         ln_last(13)

@@ -441,8 +441,8 @@ def tile_joint_t_kernel(tc, h_pred, h_enc, W1, b1, W2, b2, out):
                 xg_tile(s, 0)
                 dst, src = xgs[(s, 0)][:, :hi, :], xps[(s, 0)][:, :, :hi]
                 nc.gpsimd.tensor_scalar(
-                    out=dst.rearrange("p (c i) t -> p c t i", i=4),
-                    in0=src.rearrange("p t (c i) -> p c t i", i=4),
+                    out=dst,
+                    in0=src.rearrange("p t r -> p r t"),
                     scalar1=1.0,
                     scalar2=0.0,
                     op0=ALU.mult,

@@ -22,10 +22,15 @@ LN_OFFSET = -127.0 * 355.0 / 512.0 + 61.0 / 2048.0
 CUBE3 = 3.0 ** (1.0 / 3.0)
 W1_PIECES = ((0, 128), (128, 128), (256, 256), (512, 256), (768, 256))
 HE_PIECES = ((0, 16), (16, 16), (32, 32), (64, 64), (128, 64), (192, 64))
-GSHARE = 256
-GFIRST = 2
-SUB_AT = 0
-SHARE = 112
+SHARE1 = 384
+SHARE2 = 256
+SHARE15 = 320
+VSUB = 1
+V12 = True
+GSHARE = 0
+GFIRST = 99
+SUB_AT = 3
+SHARE = 208
 FINE = (15,)
 
 
@@ -191,14 +196,24 @@ def tile_joint_t_kernel(tc, h_pred, h_enc, W1, b1, W2, b2, out):
             nc.vector.tensor_copy(out=dst, in_=src)
             quant_he(piece)
 
+        def s_he(piece):
+            r0, nr = HE_PIECES[piece]
+            a, q0 = r0 // P, r0 % P
+            ng = nr * 3 // 4
+            nc.scalar.copy(
+                out=he_g[:, r0 + ng : r0 + nr, :, :],
+                in_=he_lin[:, a, :, q0 + ng : q0 + nr].rearrange("p t r -> p r t").unsqueeze(2).to_broadcast([P, nr - ng, 8, 4]),
+            )
+
         def hand_over(piece):
             r0, nr = HE_PIECES[piece]
             a, q0 = r0 // P, r0 % P
             hand = prep.tile([P, 4, 64], BF16, tag="hand", bufs=2, name="hand%d" % piece)
-            nc.vector.tensor_copy(out=hand[:, :, :nr], in_=he_lin[:, a, :, q0 : q0 + nr])
+            ng = nr * 3 // 4
+            nc.vector.tensor_copy(out=hand[:, :, :ng], in_=he_lin[:, a, :, q0 : q0 + ng])
             nc.gpsimd.tensor_scalar(
-                out=he_g[:, r0 : r0 + nr, :, :],
-                in0=hand[:, :, :nr].rearrange("p t r -> p r t").unsqueeze(2).to_broadcast([P, nr, 8, 4]),
+                out=he_g[:, r0 : r0 + ng, :, :],
+                in0=hand[:, :, :ng].rearrange("p t r -> p r t").unsqueeze(2).to_broadcast([P, ng, 8, 4]),
                 scalar1=1.0,
                 scalar2=0.0,
                 op0=ALU.mult,
@@ -266,17 +281,17 @@ def tile_joint_t_kernel(tc, h_pred, h_enc, W1, b1, W2, b2, out):
                 if True:
                     cols = slice(P * c, P * (c + 1))
                     zt = zps.tile([P, 512], F32, tag="z", name="z%d_%d" % (s, c))
+                    nc.tensor.matmul_mx(
+                        out=zt[:],
+                        lhsT=w1c[:, 0, cols].bitcast(FP8X4),
+                        lhsT_scale=w1s[:, 0, cols],
+                        rhs=pf_c[:].bitcast(FP8X4),
+                        rhs_scale=pf_s[:],
+                        start=True,
+                        stop=False,
+                    )
                     for a in range(4):
                         part = slice(P * a, P * (a + 1))
-                        nc.tensor.matmul_mx(
-                            out=zt[:, part],
-                            lhsT=w1c[:, 0, cols].bitcast(FP8X4),
-                            lhsT_scale=w1s[:, 0, cols],
-                            rhs=pf_c[:, part].bitcast(FP8X4),
-                            rhs_scale=pf_s[:, part],
-                            start=True,
-                            stop=False,
-                        )
                         nc.tensor.matmul_mx(
                             out=zt[:, part],
                             lhsT=w1c[:, 1, cols].bitcast(FP8X4),
@@ -284,7 +299,7 @@ def tile_joint_t_kernel(tc, h_pred, h_enc, W1, b1, W2, b2, out):
                             rhs=he8_c[:, enc].bitcast(FP8X4),
                             rhs_scale=he8_s[:, enc],
                             start=False,
-                            stop=True,
+                            stop=(a == 3),
                         )
                     nc.scalar.activation(
                         out=xp[:, tq, :].rearrange("p (t a w) -> p t a w", a=4, w=8),
@@ -348,9 +363,8 @@ def tile_joint_t_kernel(tc, h_pred, h_enc, W1, b1, W2, b2, out):
             nc.sync.dma_start(out=out_rows[512 * b : 512 * (b + 1), :].rearrange("(r p) v -> p r v", p=P), in_=ltiles[b][:])
 
         def finish_gp(b):
-            for r in range(4):
+            for r in range(4 - VSUB):
                 sub_g(b, r)
-            store(b)
 
         def sub_s(b, r):
             lt = ltiles[b]
@@ -433,7 +447,8 @@ def tile_joint_t_kernel(tc, h_pred, h_enc, W1, b1, W2, b2, out):
             if g == 0 and (s, 0) not in xgs:
                 xg_tile(s, 0)
             lo = share(s) if g == 1 else gshare(s)
-            regroup(nc.vector.tensor_copy, xgs[(s, g)][:, lo:, :], xps[(s, g)][:, :, lo:])
+            if lo < 512:
+                regroup(nc.vector.tensor_copy, xgs[(s, g)][:, lo:, :], xps[(s, g)][:, :, lo:])
 
         def g_regroup(s):
             hi = gshare(s)
@@ -441,8 +456,8 @@ def tile_joint_t_kernel(tc, h_pred, h_enc, W1, b1, W2, b2, out):
                 xg_tile(s, 0)
                 dst, src = xgs[(s, 0)][:, :hi, :], xps[(s, 0)][:, :, :hi]
                 nc.gpsimd.tensor_scalar(
-                    out=dst,
-                    in0=src.rearrange("p t r -> p r t"),
+                    out=dst.rearrange("p (c i) t -> p c t i", i=4),
+                    in0=src.rearrange("p t (c i) -> p c t i", i=4),
                     scalar1=1.0,
                     scalar2=0.0,
                     op0=ALU.mult,
@@ -453,7 +468,7 @@ def tile_joint_t_kernel(tc, h_pred, h_enc, W1, b1, W2, b2, out):
             return GSHARE if s >= GFIRST else 0
 
         def share(s):
-            return SHARE if s >= 1 else 0
+            return 0 if s == 0 else SHARE1 if s == 1 else SHARE2 if s <= 3 else SHARE if s < 15 else SHARE15
 
         def s_regroup(s):
             if s >= BLOCKS:
@@ -513,6 +528,8 @@ def tile_joint_t_kernel(tc, h_pred, h_enc, W1, b1, W2, b2, out):
                 z_tanh(s, c)
             s_regroup(s)
         for s in range(BLOCKS):
+            if 1 <= s <= 3:
+                s_he(s + 2)
             if s >= 1:
                 for c in range(4, 8):
                     z_tanh(s + 1, c)
@@ -541,26 +558,28 @@ def tile_joint_t_kernel(tc, h_pred, h_enc, W1, b1, W2, b2, out):
                 quant_he(s + 1)
             if s == BLOCKS - 1:
                 break
-            if 1 <= s <= 3:
-                hand_over(s + 2)
             for r in range(4):
-                if r == SUB_AT and s >= 5:
-                    ln_last(s - 5)
-                    finish_gp(s - 5)
-                if r == 0:
-                    g_regroup(s + 1)
                 v_bias(b, r)
                 logits(s, r)
                 z_tanh(s + 2, r)
                 if r == 0 and s >= 4 and s % 2 == 0:
                     guess_again(s - 4, s - 2)
                 run(steps)
+            if s >= 5:
+                ln_last(s - 5)
+                finish_gp(s - 5)
+            if 1 <= s <= 3:
+                hand_over(s + 2)
             v_max_block(b)
+            if s >= 5:
+                for r in range(4 - VSUB, 4):
+                    sub_v(s - 5, r)
+                store(s - 5)
             moves(s + 3)
         guess(12, 14)
         steps = stage1(12, 14)
-        for bb in (10, 11):
-            ln_last(bb)
+        ln_last(10)
+        ln_last(11)
         finish_s(10)
         for r in range(4):
             v_bias(14, r)
@@ -572,33 +591,28 @@ def tile_joint_t_kernel(tc, h_pred, h_enc, W1, b1, W2, b2, out):
         for r in range(4):
             v_max_tile(14, r)
             run(steps)
-        v_bias(15, 0)
         ln_last(12)
         ln_last(13)
-        finish_gp(12)
-        for r in (2, 3):
-            sub_g(13, r)
         exps(14)
         guess(14, 15)
-        sub_s(13, 0)
-        v_bias(15, 1)
-        v_max_tile(15, 0)
-        v_bias(15, 2)
-        v_max_tile(15, 1)
-        v_bias(15, 3)
+        finish_s(13)
+        for r in range(4):
+            v_bias(15, r)
+        if V12:
+            for r in range(4):
+                sub_v(12, r)
+            store(12)
         steps = stage1(14, 15)
-        run(steps)
-        v_max_tile(15, 2)
-        run(steps)
-        v_max_tile(15, 3)
-        run(steps)
-        run(steps)
-        exps(15, (0,))
-        sub_s(13, 1)
-        store(13)
-        exps(15, (1, 2))
-        guess_again(14, 15)
-        exps(15, (3,))
+        for r in range(4):
+            v_max_tile(15, r)
+            run(steps)
+            if r == 3:
+                guess_again(14, 15)
+            exps(15, (r,))
+        if not V12:
+            for r in range(4):
+                sub_v(12, r)
+            store(12)
         for step in stage2(14, 15):
             step()
         ln_last(14)

@@ -25,12 +25,11 @@ HE_PIECES = ((0, 16), (16, 16), (32, 32), (64, 64), (128, 64), (192, 64))
 SHARE1 = 384
 SHARE2 = 256
 SHARE15 = 320
-VSUB = 1
-V12 = True
+VSUB = 0
 GSHARE = 0
 GFIRST = 99
 SUB_AT = 3
-SHARE = 208
+SHARE = 144
 FINE = (15,)
 
 
@@ -196,11 +195,11 @@ def tile_joint_t_kernel(tc, h_pred, h_enc, W1, b1, W2, b2, out):
             nc.vector.tensor_copy(out=dst, in_=src)
             quant_he(piece)
 
-        def s_he(piece):
+        def he_rest(piece):
             r0, nr = HE_PIECES[piece]
             a, q0 = r0 // P, r0 % P
             ng = nr * 3 // 4
-            nc.scalar.copy(
+            nc.vector.tensor_copy(
                 out=he_g[:, r0 + ng : r0 + nr, :, :],
                 in_=he_lin[:, a, :, q0 + ng : q0 + nr].rearrange("p t r -> p r t").unsqueeze(2).to_broadcast([P, nr - ng, 8, 4]),
             )
@@ -353,10 +352,13 @@ def tile_joint_t_kernel(tc, h_pred, h_enc, W1, b1, W2, b2, out):
                 out=negc_blocks[b][:], in0=lng[:, cols], scalar=11.0 / 6.0, in1=lny[:, cols], op0=ALU.add, op1=ALU.add
             )
 
+        def negc(b, r):
+            return negc_blocks[b][:, r : r + 1]
+
         def sub_g(b, r):
             lt = ltiles[b]
             nc.gpsimd.tensor_scalar(
-                out=lt[:, r, :], in0=lt[:, r, :], scalar1=1.0, scalar2=negc_blocks[b][:, r : r + 1], op0=ALU.mult, op1=ALU.add
+                out=lt[:, r, :], in0=lt[:, r, :], scalar1=1.0, scalar2=negc(b, r), op0=ALU.mult, op1=ALU.add
             )
 
         def store(b):
@@ -369,13 +371,13 @@ def tile_joint_t_kernel(tc, h_pred, h_enc, W1, b1, W2, b2, out):
         def sub_s(b, r):
             lt = ltiles[b]
             nc.scalar.activation(
-                out=lt[:, r, :], in_=lt[:, r, :], func=ACT.Identity, bias=negc_blocks[b][:, r : r + 1], scale=1.0
+                out=lt[:, r, :], in_=lt[:, r, :], func=ACT.Identity, bias=negc(b, r), scale=1.0
             )
 
         def sub_v(b, r):
             lt = ltiles[b]
             nc.vector.tensor_scalar(
-                out=lt[:, r, :], in0=lt[:, r, :], scalar1=1.0, scalar2=negc_blocks[b][:, r : r + 1], op0=ALU.mult, op1=ALU.add
+                out=lt[:, r, :], in0=lt[:, r, :], scalar1=1.0, scalar2=negc(b, r), op0=ALU.mult, op1=ALU.add
             )
 
         def store_half(b, q):
@@ -402,7 +404,7 @@ def tile_joint_t_kernel(tc, h_pred, h_enc, W1, b1, W2, b2, out):
             for q in range(2):
                 for r in (2 * q, 2 * q + 1):
                     nc.vector.tensor_scalar(
-                        out=lt[:, r, :], in0=lt[:, r, :], scalar1=1.0, scalar2=negc_blocks[b][:, r : r + 1], op0=ALU.mult, op1=ALU.add
+                        out=lt[:, r, :], in0=lt[:, r, :], scalar1=1.0, scalar2=negc(b, r), op0=ALU.mult, op1=ALU.add
                     )
                 base = 512 * b + 256 * q
                 nc.sync.dma_start(
@@ -528,8 +530,6 @@ def tile_joint_t_kernel(tc, h_pred, h_enc, W1, b1, W2, b2, out):
                 z_tanh(s, c)
             s_regroup(s)
         for s in range(BLOCKS):
-            if 1 <= s <= 3:
-                s_he(s + 2)
             if s >= 1:
                 for c in range(4, 8):
                     z_tanh(s + 1, c)
@@ -542,6 +542,10 @@ def tile_joint_t_kernel(tc, h_pred, h_enc, W1, b1, W2, b2, out):
             steps = iter_steps(s)
             v_regroup(s, 0)
             run(steps)
+            if 2 <= s <= 4:
+                he_rest(s + 1)
+            if s == 0:
+                regroup(nc.vector.tensor_copy, w2g[0][:], w2raw[0][:])
             v_regroup(s, 1)
             run(steps)
             v_quant(s, 0)
@@ -550,8 +554,9 @@ def tile_joint_t_kernel(tc, h_pred, h_enc, W1, b1, W2, b2, out):
             run(steps)
             if s == 0:
                 v_he(2)
-                for g in range(2):
-                    regroup(nc.vector.tensor_copy, w2g[g][:], w2raw[g][:])
+                for c in range(4):
+                    z_tanh(2, c)
+                regroup(nc.vector.tensor_copy, w2g[1][:], w2raw[1][:])
                 quant_w2(0)
                 quant_w2(1)
             if 2 <= s <= 4:
@@ -559,17 +564,18 @@ def tile_joint_t_kernel(tc, h_pred, h_enc, W1, b1, W2, b2, out):
             if s == BLOCKS - 1:
                 break
             for r in range(4):
+                if r == 3 and s >= 5:
+                    ln_last(s - 5)
+                    finish_gp(s - 5)
+                if r == 3 and 1 <= s <= 3:
+                    hand_over(s + 2)
                 v_bias(b, r)
                 logits(s, r)
-                z_tanh(s + 2, r)
+                if s >= 1:
+                    z_tanh(s + 2, r)
                 if r == 0 and s >= 4 and s % 2 == 0:
                     guess_again(s - 4, s - 2)
                 run(steps)
-            if s >= 5:
-                ln_last(s - 5)
-                finish_gp(s - 5)
-            if 1 <= s <= 3:
-                hand_over(s + 2)
             v_max_block(b)
             if s >= 5:
                 for r in range(4 - VSUB, 4):
@@ -593,26 +599,24 @@ def tile_joint_t_kernel(tc, h_pred, h_enc, W1, b1, W2, b2, out):
             run(steps)
         ln_last(12)
         ln_last(13)
+        for r in range(4):
+            sub_v(12, r)
+        store(12)
         exps(14)
         guess(14, 15)
-        finish_s(13)
+        for r in range(4):
+            sub_s(13, r)
+            if r % 2 == 1:
+                store_half(13, r // 2)
         for r in range(4):
             v_bias(15, r)
-        if V12:
-            for r in range(4):
-                sub_v(12, r)
-            store(12)
         steps = stage1(14, 15)
         for r in range(4):
-            v_max_tile(15, r)
             run(steps)
+            v_max_tile(15, r)
             if r == 3:
                 guess_again(14, 15)
             exps(15, (r,))
-        if not V12:
-            for r in range(4):
-                sub_v(12, r)
-            store(12)
         for step in stage2(14, 15):
             step()
         ln_last(14)

@@ -564,7 +564,7 @@ def tile_joint_t_kernel(tc, h_pred, h_enc, W1, b1, W2, b2, out):
             if s == BLOCKS - 1:
                 break
             for r in range(4):
-                if r == 3 and s >= 5:
+                if r == 2 and s >= 5:
                     ln_last(s - 5)
                     finish_gp(s - 5)
                 if r == 3 and 1 <= s <= 3:

@@ -195,20 +195,11 @@ def tile_joint_t_kernel(tc, h_pred, h_enc, W1, b1, W2, b2, out):
             nc.vector.tensor_copy(out=dst, in_=src)
             quant_he(piece)
 
-        def he_rest(piece):
-            r0, nr = HE_PIECES[piece]
-            a, q0 = r0 // P, r0 % P
-            ng = nr * 3 // 4
-            nc.vector.tensor_copy(
-                out=he_g[:, r0 + ng : r0 + nr, :, :],
-                in_=he_lin[:, a, :, q0 + ng : q0 + nr].rearrange("p t r -> p r t").unsqueeze(2).to_broadcast([P, nr - ng, 8, 4]),
-            )
-
         def hand_over(piece):
             r0, nr = HE_PIECES[piece]
             a, q0 = r0 // P, r0 % P
             hand = prep.tile([P, 4, 64], BF16, tag="hand", bufs=2, name="hand%d" % piece)
-            ng = nr * 3 // 4
+            ng = nr
             nc.vector.tensor_copy(out=hand[:, :, :ng], in_=he_lin[:, a, :, q0 : q0 + ng])
             nc.gpsimd.tensor_scalar(
                 out=he_g[:, r0 : r0 + ng, :, :],
@@ -542,8 +533,6 @@ def tile_joint_t_kernel(tc, h_pred, h_enc, W1, b1, W2, b2, out):
             steps = iter_steps(s)
             v_regroup(s, 0)
             run(steps)
-            if 2 <= s <= 4:
-                he_rest(s + 1)
             if s == 0:
                 regroup(nc.vector.tensor_copy, w2g[0][:], w2raw[0][:])
             v_regroup(s, 1)
@@ -564,10 +553,10 @@ def tile_joint_t_kernel(tc, h_pred, h_enc, W1, b1, W2, b2, out):
             if s == BLOCKS - 1:
                 break
             for r in range(4):
-                if r == 2 and s >= 5:
+                if r == 0 and s >= 5:
                     ln_last(s - 5)
                     finish_gp(s - 5)
-                if r == 3 and 1 <= s <= 3:
+                if r == 0 and 1 <= s <= 3:
                     hand_over(s + 2)
                 v_bias(b, r)
                 logits(s, r)

from contextlib import ExitStack

import concourse.mybir as mybir
from concourse.masks import make_identity

FLOPS = 2 * (128 * 512 * 1024 + 256 * 512 * 1024 + 8192 * 1024 * 512)

BF16 = mybir.dt.bfloat16
F32 = mybir.dt.float32
U32 = mybir.dt.uint32
I32 = mybir.dt.int32
U8 = mybir.dt.uint8
FP8X4 = mybir.dt.float8_e4m3fn_x4
ACT = mybir.ActivationFunctionType
ALU = mybir.AluOpType
AX = mybir.AxisListType

P = 128
BLOCKS = 16
LN_SLOPE = 355.0 / 512.0 / 2.0**23
LN_OFFSET = -127.0 * 355.0 / 512.0 + 61.0 / 2048.0
CUBE3 = 3.0 ** (1.0 / 3.0)
W1_PIECES = ((0, 128), (128, 128), (256, 256), (512, 256), (768, 256))
HE_PIECES = ((0, 16), (16, 16), (32, 32), (64, 64), (128, 64), (192, 64))
SHARE1 = 384
SHARE2 = 256
SHARE15 = 320
VSUB = 0
GSHARE = 0
GFIRST = 99
SUB_AT = 3
SHARE = 144
FINE = (15,)


def regroup(engine_copy, dst, src):
    engine_copy(
        out=dst.rearrange("p (c i) t -> p c t i", i=4),
        in_=src.rearrange("p t (c i) -> p c t i", i=4),
    )


def tile_joint_t_kernel(tc, h_pred, h_enc, W1, b1, W2, b2, out):
    nc = tc.nc
    out_rows = out.flatten_outer_dims()
    with ExitStack() as ctx:
        ctx.enter_context(tc.manual_schedule())
        const = ctx.enter_context(tc.tile_pool(name="const", bufs=1))
        prep = ctx.enter_context(tc.tile_pool(name="prep", bufs=1))
        loop = ctx.enter_context(tc.tile_pool(name="loop", bufs=2))
        lpool = ctx.enter_context(tc.tile_pool(name="lpool", bufs=9))

        b1t = prep.tile([P, P], BF16)
        nc.vector.memset(b1t[:], 0.0)
        warm = const.tile([P, 1], F32)
        nc.vector.memset(warm[:], 0.0)
        hp_s = const.tile([P, 128], U8, align_bytes=64)
        he8_s = const.tile([P, 2048], U8, align_bytes=64)
        nc.vector.memset(hp_s[:].bitcast(I32), 0)

        w1raw = {}

        def load_w1(h):
            j0, jw = W1_PIECES[h]
            for g in range(2):
                raw = prep.tile([P, 4, jw], BF16, name="w1raw%d%d" % (g, h))
                nc.sync.dma_start(
                    out=raw[:],
                    in_=W1[512 * g : 512 * (g + 1), j0 : j0 + jw].rearrange("(t p) j -> p t j", p=P),
                )
                w1raw[(g, h)] = raw

        he_sb = prep.tile([P, 2, 512], BF16)
        he_rows = h_enc.flatten_outer_dims().rearrange("(a p) k -> p a k", p=P)
        hp_sb = prep.tile([P, 512], BF16)
        nc.sync.dma_start(out=he_sb[:, 0, :], in_=he_rows[:, 0, :])
        load_w1(0)
        nc.sync.dma_start(out=hp_sb[:], in_=h_pred.flatten_outer_dims())
        nc.sync.dma_start(out=b1t[0:8, :], in_=b1.rearrange("(c p) -> c p", p=P))
        load_w1(1)
        nc.sync.dma_start(out=he_sb[:, 1, :], in_=he_rows[:, 1, :])
        load_w1(2)
        load_w1(3)
        load_w1(4)
        w2raw = {}
        for g in range(2):
            raw = prep.tile([P, 4, 512], BF16, tag="w2raw", bufs=2, name="w2raw%d" % g)
            nc.sync.dma_start(out=raw[:], in_=W2[512 * g : 512 * (g + 1), :].rearrange("(t p) v -> p t v", p=P))
            w2raw[g] = raw
        b2b = prep.tile([P, 512], BF16)
        nc.sync.dma_start(out=b2b[:], in_=b2.partition_broadcast(P))

        warm2 = const.tile([P, 1], F32)
        nc.scalar.activation(out=warm2[:], in_=warm[:], func=ACT.Tanh)
        ident = const.tile([P, P], BF16)
        make_identity(nc, ident[:])

        w1c = const.tile([P, 2, 1024], U32, align_bytes=64)
        w1s = const.tile([P, 2, 1024], U8, align_bytes=64)
        w2c = const.tile([P, 2, 512], U32, align_bytes=64)
        w2s = const.tile([P, 2, 512], U8, align_bytes=64)
        hp_c = const.tile([P, 128], U32, align_bytes=64)
        he8_c = const.tile([P, 2048], U32, align_bytes=64)
        b1_sb = const.tile([P, 8], F32)
        negm = const.tile([P, 64], F32)
        ssum = const.tile([P, 64], F32)
        lny = const.tile([P, 64], F32)
        lne = const.tile([P, 64], F32)
        lnt = const.tile([P, 64], F32)
        lnb = const.tile([P, 64], F32)
        lng = const.tile([P, 64], F32)
        negc_blocks = [const.tile([P, 4], F32, name="negc%d" % b) for b in range(BLOCKS)]
        ebias = const.tile([P, 1], F32)
        nc.vector.memset(ebias[:], -LN_OFFSET)

        he_g = prep.tile([P, 256, 8, 4], BF16, align_bytes=64)
        he_lin = prep.tile([P, 2, 4, P], BF16)
        hp_g = prep.tile([P, P, 4], BF16, align_bytes=64)
        w1g = {}
        for h, (j0, jw) in enumerate(W1_PIECES):
            for g in range(2):
                w1g[(g, h)] = prep.tile([P, jw, 4], BF16, align_bytes=64, name="w1g%d%d" % (g, h))
        with tc.psum_pool(name="pps", bufs=1) as pps:
            heT = pps.tile([P, 2, 4, P], BF16)
            hpT = pps.tile([P, 4, P], BF16)
            b1T = pps.tile([P, P], BF16)
            for t in range(4):
                nc.tensor.transpose(heT[:, 0, t, :], he_sb[:, 0, P * t : P * (t + 1)], ident[:])
            for t in range(4):
                nc.tensor.transpose(hpT[:, t, :], hp_sb[:, P * t : P * (t + 1)], ident[:])
            nc.tensor.transpose(b1T[:], b1t[:], ident[:])
            nc.scalar.copy(out=he_lin[:, 0], in_=heT[:, 0])
            nc.scalar.copy(out=hp_g[:], in_=hpT[:].rearrange("p t r -> p r t"))
            nc.scalar.copy(out=b1_sb[:], in_=b1T[:, 0:8])
            regroup(nc.scalar.copy, w1g[(1, 1)][:], w1raw[(1, 1)][:])
            for t in range(4):
                nc.tensor.transpose(heT[:, 1, t, :], he_sb[:, 1, P * t : P * (t + 1)], ident[:])
            nc.scalar.copy(out=he_lin[:, 1], in_=heT[:, 1])
            regroup(nc.scalar.copy, w1g[(1, 2)][:], w1raw[(1, 2)][:])
            regroup(nc.scalar.copy, w1g[(1, 3)][:], w1raw[(1, 3)][:])

        def he_views(piece):
            r0, nr = HE_PIECES[piece]
            a, q0 = r0 // P, r0 % P
            dst = he_g[:, r0 : r0 + nr, :, :]
            src = (
                he_lin[:, a, :, q0 : q0 + nr].rearrange("p t r -> p r t").unsqueeze(2).to_broadcast([P, nr, 8, 4])
            )
            return dst, src

        def quant_he(piece):
            r0, nr = HE_PIECES[piece]
            nc.vector.quantize_mx(
                out=he8_c[:, 8 * r0 : 8 * (r0 + nr)].bitcast(FP8X4),
                scales=he8_s[:, 8 * r0 : 8 * (r0 + nr)],
                in_=he_g[:, r0 : r0 + nr].rearrange("p r e t -> p (r e t)"),
            )

        pf = {}

        def moves(b):
            if b >= BLOCKS or b % 4 != 0:
                return
            n = b // 4
            pf_c = const.tile([P, 512], U32, align_bytes=64, name="pfc%d" % n)
            pf_s = const.tile([P, 512], U8, align_bytes=64, name="pfs%d" % n)
            nc.vector.tensor_copy(
                out=pf_c[:].bitcast(I32).rearrange("p (a t w) -> p a t w", a=4, w=8),
                in_=hp_c[:, 32 * n : 32 * (n + 1)]
                .bitcast(I32)
                .rearrange("p (a w) -> p a w", w=8)
                .unsqueeze(2)
                .to_broadcast([P, 4, 16, 8]),
            )
            nc.vector.tensor_copy(
                out=pf_s[:].bitcast(I32).rearrange("p (a t w) -> p a t w", a=4, w=2),
                in_=hp_s[:, 32 * n : 32 * (n + 1)]
                .bitcast(I32)
                .rearrange("p (a w) -> p a w", w=2)
                .unsqueeze(2)
                .to_broadcast([P, 4, 16, 2]),
            )
            pf[n] = (pf_c, pf_s)

        def quant_w1(g, h):
            j0, jw = W1_PIECES[h]
            nc.vector.quantize_mx(
                out=w1c[:, g, j0 : j0 + jw].bitcast(FP8X4),
                scales=w1s[:, g, j0 : j0 + jw],
                in_=w1g[(g, h)][:].rearrange("p w t -> p (w t)"),
            )

        def v_he(piece):
            dst, src = he_views(piece)
            nc.vector.tensor_copy(out=dst, in_=src)
            quant_he(piece)

        def hand_over(piece):
            r0, nr = HE_PIECES[piece]
            a, q0 = r0 // P, r0 % P
            hand = prep.tile([P, 4, 64], BF16, tag="hand", bufs=2, name="hand%d" % piece)
            ng = nr
            nc.vector.tensor_copy(out=hand[:, :, :ng], in_=he_lin[:, a, :, q0 : q0 + ng])
            nc.gpsimd.tensor_scalar(
                out=he_g[:, r0 : r0 + ng, :, :],
                in0=hand[:, :, :ng].rearrange("p t r -> p r t").unsqueeze(2).to_broadcast([P, ng, 8, 4]),
                scalar1=1.0,
                scalar2=0.0,
                op0=ALU.mult,
                op1=ALU.add,
            )

        def quant_w2(g):
            nc.vector.quantize_mx(
                out=w2c[:, g, :].bitcast(FP8X4),
                scales=w2s[:, g, :],
                in_=w2g[g][:].rearrange("p w t -> p (w t)"),
            )

        def v_w1(g, h):
            regroup(nc.vector.tensor_copy, w1g[(g, h)][:], w1raw[(g, h)][:])

        w2g = {}
        for g in range(2):
            w2g[g] = prep.tile([P, 512, 4], BF16, tag="w2g", bufs=2, align_bytes=64, name="w2g%d" % g)

        v_w1(0, 0)
        v_w1(1, 0)
        quant_w1(0, 0)
        quant_w1(1, 0)
        dst, src = he_views(0)
        nc.vector.tensor_copy(out=dst, in_=src)
        nc.vector.quantize_mx(
            out=hp_c[:].bitcast(FP8X4), scales=hp_s[:], in_=hp_g[:].rearrange("p r t -> p (r t)")
        )
        quant_he(0)
        moves(0)
        v_w1(0, 1)
        v_w1(0, 2)
        quant_w1(0, 1)
        quant_w1(1, 1)
        v_w1(0, 3)
        quant_w1(0, 2)
        quant_w1(1, 2)
        v_w1(0, 4)
        v_w1(1, 4)
        quant_w1(0, 3)
        quant_w1(1, 3)
        quant_w1(0, 4)
        quant_w1(1, 4)
        v_he(1)

        zps = ctx.enter_context(tc.psum_pool(name="zps", bufs=4))
        lps = ctx.enter_context(tc.psum_pool(name="lps", bufs=4))

        xps = {}
        xgs = {}
        xq = {}
        accs = {}
        ltiles = {}

        def z_tanh(s, c):
                if s >= BLOCKS:
                    return
                pf_c, pf_s = pf[s // 4]
                enc = slice(P * s, P * (s + 1))
                g, tq = c // 4, c % 4
                if tq == 0:
                    xps[(s, g)] = loop.tile([P, 4, 512], BF16, tag="xp", bufs=4, name="xp%d_%d" % (s, g))
                xp = xps[(s, g)]
                if True:
                    cols = slice(P * c, P * (c + 1))
                    zt = zps.tile([P, 512], F32, tag="z", name="z%d_%d" % (s, c))
                    nc.tensor.matmul_mx(
                        out=zt[:],
                        lhsT=w1c[:, 0, cols].bitcast(FP8X4),
                        lhsT_scale=w1s[:, 0, cols],
                        rhs=pf_c[:].bitcast(FP8X4),
                        rhs_scale=pf_s[:],
                        start=True,
                        stop=False,
                    )
                    for a in range(4):
                        part = slice(P * a, P * (a + 1))
                        nc.tensor.matmul_mx(
                            out=zt[:, part],
                            lhsT=w1c[:, 1, cols].bitcast(FP8X4),
                            lhsT_scale=w1s[:, 1, cols],
                            rhs=he8_c[:, enc].bitcast(FP8X4),
                            rhs_scale=he8_s[:, enc],
                            start=False,
                            stop=(a == 3),
                        )
                    nc.scalar.activation(
                        out=xp[:, tq, :].rearrange("p (t a w) -> p t a w", a=4, w=8),
                        in_=zt[:].rearrange("p (a t w) -> p t a w", a=4, w=8),
                        func=ACT.Tanh,
                        bias=b1_sb[:, c : c + 1],
                        scale=1.0,
                    )

        def guess(lo, hi):
            cols = slice(4 * lo, 4 * hi)
            bits = ssum[:, cols].bitcast(U32)
            nc.scalar.activation(out=lny[:, cols], in_=bits, func=ACT.Identity, bias=ebias[:], scale=-LN_SLOPE)
            nc.scalar.activation(out=lne[:, cols], in_=bits, func=ACT.Exp, bias=ebias[:], scale=-LN_SLOPE)

        def guess_again(lo, hi):
            cols = slice(4 * lo, 4 * hi)
            nc.scalar.activation(out=lne[:, cols], in_=lnb[:, cols], func=ACT.Exp, scale=1.0)

        def ln_poly(lo, hi):
            cols = slice(4 * lo, 4 * hi)
            t, g, e = lnt[:, cols], lng[:, cols], lne[:, cols]
            stt = nc.vector.scalar_tensor_tensor
            return [
                lambda: stt(out=t, in0=ssum[:, cols], scalar=-1.0 / CUBE3, in1=e, op0=ALU.mult, op1=ALU.mult),
                lambda: stt(out=g, in0=t, scalar=1.5 * CUBE3 * CUBE3, in1=t, op0=ALU.add, op1=ALU.mult),
                lambda: stt(out=g, in0=g, scalar=3.0 * CUBE3, in1=t, op0=ALU.add, op1=ALU.mult),
            ]

        def stage1(lo, hi):
            cols = slice(4 * lo, 4 * hi)
            return ln_poly(lo, hi) + [
                lambda: nc.vector.scalar_tensor_tensor(
                    out=lnb[:, cols], in0=lng[:, cols], scalar=11.0 / 6.0, in1=lny[:, cols], op0=ALU.add, op1=ALU.add
                )
            ]

        def stage2(lo, hi):
            cols = slice(4 * lo, 4 * hi)
            p = ln_poly(lo, hi)
            return [
                p[0],
                lambda: nc.vector.tensor_tensor(out=lny[:, cols], in0=lnb[:, cols], in1=negm[:, cols], op=ALU.add),
                p[1],
                p[2],
            ]

        def ln_last(b):
            cols = slice(4 * b, 4 * (b + 1))
            nc.vector.scalar_tensor_tensor(
                out=negc_blocks[b][:], in0=lng[:, cols], scalar=11.0 / 6.0, in1=lny[:, cols], op0=ALU.add, op1=ALU.add
            )

        def negc(b, r):
            return negc_blocks[b][:, r : r + 1]

        def sub_g(b, r):
            lt = ltiles[b]
            nc.gpsimd.tensor_scalar(
                out=lt[:, r, :], in0=lt[:, r, :], scalar1=1.0, scalar2=negc(b, r), op0=ALU.mult, op1=ALU.add
            )

        def store(b):
            nc.sync.dma_start(out=out_rows[512 * b : 512 * (b + 1), :].rearrange("(r p) v -> p r v", p=P), in_=ltiles[b][:])

        def finish_gp(b):
            for r in range(4 - VSUB):
                sub_g(b, r)

        def sub_s(b, r):
            lt = ltiles[b]
            nc.scalar.activation(
                out=lt[:, r, :], in_=lt[:, r, :], func=ACT.Identity, bias=negc(b, r), scale=1.0
            )

        def sub_v(b, r):
            lt = ltiles[b]
            nc.vector.tensor_scalar(
                out=lt[:, r, :], in0=lt[:, r, :], scalar1=1.0, scalar2=negc(b, r), op0=ALU.mult, op1=ALU.add
            )

        def store_half(b, q):
            base = 512 * b + 256 * q
            nc.sync.dma_start(
                out=out_rows[base : base + 256, :].rearrange("(r p) v -> p r v", p=P), in_=ltiles[b][:, 2 * q : 2 * q + 2, :]
            )

        def finish_s(b):
            for r in range(4):
                sub_s(b, r)
            store(b)

        def finish_both(b):
            for r in (2, 3):
                sub_s(b, r)
            for r in (0, 1):
                sub_v(b, r)
            store_half(b, 0)
            store_half(b, 1)

        def finish_v(b):
            lt = ltiles[b]
            for q in range(2):
                for r in (2 * q, 2 * q + 1):
                    nc.vector.tensor_scalar(
                        out=lt[:, r, :], in0=lt[:, r, :], scalar1=1.0, scalar2=negc(b, r), op0=ALU.mult, op1=ALU.add
                    )
                base = 512 * b + 256 * q
                nc.sync.dma_start(
                    out=out_rows[base : base + 256, :].rearrange("(r p) v -> p r v", p=P), in_=lt[:, 2 * q : 2 * q + 2, :]
                )

        def logits(b, r):
            xc, xs = xq[b]
            if True:
                rows = slice(P * r, P * (r + 1))
                acc = lps.tile([P, 512], F32, tag="lg", name="lg%d_%d" % (b, r))
                accs[(b, r)] = acc
                for g in range(2):
                    nc.tensor.matmul_mx(
                        out=acc[:],
                        lhsT=xc[:, g, rows].bitcast(FP8X4),
                        lhsT_scale=xs[:, g, rows],
                        rhs=w2c[:, g, :].bitcast(FP8X4),
                        rhs_scale=w2s[:, g, :],
                        start=(g == 0),
                        stop=(g == 1),
                    )

        def exps(b, tiles=range(4)):
            lt = ltiles[b]
            for r in tiles:
                i = 4 * b + r
                junk = loop.tile([P, 512], BF16, tag="junk", bufs=2, name="junk%d" % i)
                nc.scalar.activation(
                    out=junk[:],
                    in_=lt[:, r, :],
                    func=ACT.Exp,
                    bias=negm[:, i : i + 1],
                    scale=1.0,
                    accum_out=ssum[:, i : i + 1],
                )

        def xg_tile(s, g):
            xgs[(s, g)] = loop.tile([P, 512, 4], BF16, tag="xg%d" % g, bufs=2, align_bytes=64, name="xg%d_%d" % (s, g))

        def v_regroup(s, g):
            if g == 0 and (s, 0) not in xgs:
                xg_tile(s, 0)
            lo = share(s) if g == 1 else gshare(s)
            if lo < 512:
                regroup(nc.vector.tensor_copy, xgs[(s, g)][:, lo:, :], xps[(s, g)][:, :, lo:])

        def g_regroup(s):
            hi = gshare(s)
            if hi:
                xg_tile(s, 0)
                dst, src = xgs[(s, 0)][:, :hi, :], xps[(s, 0)][:, :, :hi]
                nc.gpsimd.tensor_scalar(
                    out=dst.rearrange("p (c i) t -> p c t i", i=4),
                    in0=src.rearrange("p t (c i) -> p c t i", i=4),
                    scalar1=1.0,
                    scalar2=0.0,
                    op0=ALU.mult,
                    op1=ALU.add,
                )

        def gshare(s):
            return GSHARE if s >= GFIRST else 0

        def share(s):
            return 0 if s == 0 else SHARE1 if s == 1 else SHARE2 if s <= 3 else SHARE if s < 15 else SHARE15

        def s_regroup(s):
            if s >= BLOCKS:
                return
            xg_tile(s, 1)
            hi = share(s)
            if hi:
                regroup(nc.scalar.copy, xgs[(s, 1)][:, :hi, :], xps[(s, 1)][:, :, :hi])

        def v_quant(s, g):
            if s >= BLOCKS:
                return
            if g == 0:
                xc = loop.tile([P, 2, 512], U32, align_bytes=64, tag="xc", bufs=2, name="xc%d" % s)
                xs = loop.tile([P, 2, 512], U8, align_bytes=64, tag="xs", bufs=2, name="xs%d" % s)
                xq[s] = (xc, xs)
            xc, xs = xq[s]
            nc.vector.quantize_mx(
                out=xc[:, g, :].bitcast(FP8X4),
                scales=xs[:, g, :],
                in_=xgs[(s, g)][:].rearrange("p w t -> p (w t)"),
            )

        def v_bias(b, r):
            if b < 0:
                return
            if r == 0:
                ltiles[b] = lpool.tile([P, 4, 512], F32, tag="L", name="L%d" % b)
            nc.vector.tensor_tensor(out=ltiles[b][:, r, :], in0=b2b[:], in1=accs[(b, r)][:], op=ALU.add)

        def v_max_tile(b, r):
            i = 4 * b + r
            nc.vector.tensor_reduce(
                out=negm[:, i : i + 1], in_=ltiles[b][:, r, :], axis=AX.X, op=ALU.max, negate=True
            )

        def v_max_block(b):
            if b >= 0:
                for lo, hi in ((0, 3), (3, 4)):
                    nc.vector.tensor_reduce(
                        out=negm[:, 4 * b + lo : 4 * b + hi], in_=ltiles[b][:, lo:hi, :], axis=AX.X, op=ALU.max, negate=True
                    )

        def iter_steps(s):
            if s < 4:
                return []
            return stage1(s - 4, s - 2) if s % 2 == 0 else stage2(s - 5, s - 3)

        def run(steps):
            if steps:
                step = steps[0]
                steps.remove(step)
                step()

        for s in range(2):
            for c in range(8):
                z_tanh(s, c)
            s_regroup(s)
        for s in range(BLOCKS):
            if s >= 1:
                for c in range(4, 8):
                    z_tanh(s + 1, c)
                s_regroup(s + 1)
            if s >= 2:
                exps(s - 2)
            if s >= 3 and s % 2 == 1 and s < 15:
                guess(s - 3, s - 1)
            b = s - 1
            steps = iter_steps(s)
            v_regroup(s, 0)
            run(steps)
            if s == 0:
                regroup(nc.vector.tensor_copy, w2g[0][:], w2raw[0][:])
            v_regroup(s, 1)
            run(steps)
            v_quant(s, 0)
            run(steps)
            v_quant(s, 1)
            run(steps)
            if s == 0:
                v_he(2)
                for c in range(4):
                    z_tanh(2, c)
                regroup(nc.vector.tensor_copy, w2g[1][:], w2raw[1][:])
                quant_w2(0)
                quant_w2(1)
            if 2 <= s <= 4:
                quant_he(s + 1)
            if s == BLOCKS - 1:
                break
            for r in range(4):
                if r == 0 and s >= 5:
                    ln_last(s - 5)
                    finish_gp(s - 5)
                if r == 0 and 1 <= s <= 3:
                    hand_over(s + 2)
                v_bias(b, r)
                logits(s, r)
                if s >= 1:
                    z_tanh(s + 2, r)
                if r == 0 and s >= 4 and s % 2 == 0:
                    guess_again(s - 4, s - 2)
                run(steps)
            v_max_block(b)
            if s >= 5:
                for r in range(4 - VSUB, 4):
                    sub_v(s - 5, r)
                store(s - 5)
            moves(s + 3)
        guess(12, 14)
        steps = stage1(12, 14)
        ln_last(10)
        ln_last(11)
        finish_s(10)
        for r in range(4):
            v_bias(14, r)
            logits(15, r)
            run(steps)
        guess_again(12, 14)
        finish_s(11)
        steps = stage2(12, 14)
        for r in range(4):
            v_max_tile(14, r)
            run(steps)
        ln_last(12)
        ln_last(13)
        for r in range(4):
            sub_v(12, r)
        store(12)
        exps(14)
        guess(14, 15)
        for r in range(4):
            sub_s(13, r)
            if r % 2 == 1:
                store_half(13, r // 2)
        for r in range(4):
            v_bias(15, r)
        steps = stage1(14, 15)
        for r in range(4):
            run(steps)
            v_max_tile(15, r)
            if r == 3:
                guess_again(14, 15)
            exps(15, (r,))
        for step in stage2(14, 15):
            step()
        ln_last(14)
        finish_v(14)
        cols = slice(60, 64)
        nc.scalar.activation(out=lne[:, cols], in_=ssum[:, cols], func=ACT.Ln)
        nc.vector.tensor_tensor(out=negc_blocks[15][:], in0=negm[:, cols], in1=lne[:, cols], op=ALU.subtract)
        finish_both(15)
